import numpy as np
import ml_dtypes


def mxq(x, axis, fmt="e4m3"):
    dtype, down = {"e4m3": (ml_dtypes.float8_e4m3fn, 7), "e5m2": (ml_dtypes.float8_e5m2, 14)}[fmt]
    v = np.moveaxis(np.asarray(x, np.float32).astype(ml_dtypes.bfloat16).astype(np.float64), axis, -1)
    blocks = v.reshape(v.shape[:-1] + (-1, 32))
    amax = np.abs(blocks).max(-1, keepdims=True)
    byte = np.maximum(np.where(amax > 0, np.frexp(amax)[1] - 1 + 127, 0) - down, 1)
    scale = np.exp2(byte - 127.0)
    codes = (blocks / scale).astype(np.float32).astype(dtype).astype(np.float64)
    return np.moveaxis((codes * scale).reshape(v.shape), -1, axis)


WIDE = False


def mx_kscale(k):
    if not WIDE:
        return np.ones(k)
    levels = np.array([10, -10, 5, -5, 0])
    a = np.random.permutation(np.resize(levels, k // 512 * 4)).reshape(k // 512, 4)
    idx = np.arange(k)
    return np.exp2(a[idx // 512, idx % 128 // 32])


BF16 = ml_dtypes.bfloat16


def bf(x):
    return np.asarray(x, np.float32).astype(BF16)


def f64(x):
    return np.asarray(x).astype(np.float64)


E2M1 = np.array([0.0, 0.5, 1.0, 1.5, 2.0, 3.0, 4.0, 6.0, -0.0, -0.5, -1.0, -1.5, -2.0, -3.0, -4.0, -6.0])


def pack_weight(w, fmt):
    k, n = w.shape
    w = f64(bf(w)).reshape(k // 32, 32, n)
    amax = np.abs(w).max(1)
    if fmt == "e4m3":
        byte = np.frexp(amax)[1] - 1 + 127 - 7
    else:
        mant, ex = np.frexp(amax / 6.0)
        byte = np.where(mant > 0.5, ex, ex - 1) + 127
    byte = np.clip(np.where(amax > 0, byte, 1), 1, 254)
    scaled = (w * np.exp2(127.0 - byte)[:, None, :]).reshape(k, n).astype(np.float32)
    by_word = np.ascontiguousarray(scaled.reshape(k // 512, 128, 4, n).transpose(0, 1, 3, 2))
    if fmt == "e4m3":
        words = by_word.astype(ml_dtypes.float8_e4m3fn).view(np.uint8)
    else:
        c = by_word.astype(ml_dtypes.float4_e2m1fn).view(np.uint8) & 0xF
        words = c[..., 0::2] | (c[..., 1::2] << 4)
    return np.ascontiguousarray(words), np.ascontiguousarray(byte.astype(np.uint8).reshape(k // 512, 16, n))


def unpack_weight(words, scales, fmt):
    g, p, n, _ = words.shape
    if fmt == "e4m3":
        vals = np.ascontiguousarray(words).view(ml_dtypes.float8_e4m3fn).astype(np.float64)
    else:
        nib = np.empty((g, p, n, 4), np.uint8)
        nib[..., 0::2] = words & 0xF
        nib[..., 1::2] = words >> 4
        vals = E2M1[nib]
    vals = vals * np.repeat(np.exp2(scales.astype(np.float64) - 127.0), 8, axis=1)[..., None]
    return vals.transpose(0, 1, 3, 2).reshape(g * 512, n)


B, INPUT_DIM, PE_DIM, OUT_DIM = 1024, 4, 512, 4096
DPI = PE_DIM // INPUT_DIM
MAX_COORD = 10.0
LN_EPS = 1e-5
MXB = 32
J0 = DPI // 2 - 2
LO = J0 // MXB * MXB
FMT = "e4m3"


def sinusoidal_pe(s):
    j = np.arange(DPI, dtype=np.float64)
    freq = np.power(10000.0, -2.0 * j / DPI)
    angle = s[:, :, None] * freq[None, None, :]
    pe = np.where((np.arange(DPI) % 2) == 0, np.sin(angle), np.cos(angle))
    return pe.reshape(s.shape[0], PE_DIM)


def setup_inputs():
    t = mx_kscale(PE_DIM)
    a = 20.0 * float(np.max(t) > np.min(t))
    fac = np.full((INPUT_DIM, DPI), np.exp2(-a / 10))
    fac[:, LO:LO + MXB] = np.exp2(-a / 10 - a / 2)
    fac[:, J0] = np.exp2(a - a / 5)
    fac = fac.reshape(PE_DIM)
    state = bf(np.random.uniform(-0.5, 1.5, (B, INPUT_DIM)) * MAX_COORD)
    w = np.random.standard_normal((OUT_DIM, PE_DIM)) * 0.024 / np.sqrt(PE_DIM) * fac[None, :]
    words, scales = pack_weight(w.T, FMT)
    return {"state": state,
            "W_words": words,
            "W_scales": scales,
            "b": bf((0.01 + 0.01 * np.random.standard_normal(OUT_DIM)) * np.exp2(-a / 10)),
            "gamma": bf(1.0 + 0.1 * np.random.standard_normal(OUT_DIM)),
            "beta": bf(0.1 * np.random.standard_normal(OUT_DIM))}


def reference(state, W_words, W_scales, b, gamma, beta):
    s = np.clip(f64(state) / MAX_COORD, 0.0, 1.0)
    pe = sinusoidal_pe(s)
    y = (mxq(pe, 1, "e4m3") @ unpack_weight(W_words, W_scales, FMT)) + f64(b)
    mu = np.mean(y, axis=-1, keepdims=True)
    var = np.mean(np.square(y - mu), axis=-1, keepdims=True)
    return (y - mu) / np.sqrt(var + LN_EPS) * f64(gamma) + f64(beta)

@@ -1,0 +1,178 @@
+import math
+
+import concourse.mybir as mybir
+from concourse.masks import make_identity
+
+F32 = mybir.dt.float32
+BF16 = mybir.dt.bfloat16
+I32 = mybir.dt.int32
+U32 = mybir.dt.uint32
+U8 = mybir.dt.uint8
+FP8X4 = mybir.dt.float8_e4m3fn_x4
+ALU = mybir.AluOpType
+ACT = mybir.ActivationFunctionType
+AXIS = mybir.AxisListType
+
+P = 128
+PACK = 4
+ROWS = 1024
+COORDS = 4
+PER_COORD = 128
+N_OUT = 4096
+BANK = 512
+ROW_TILES = ROWS // P
+BANKS = N_OUT // BANK
+MAX_COORD = 10.0
+LN_EPS = 1e-5
+
+FLOPS = 2 * ROWS * COORDS * PER_COORD * N_OUT
+
+
+def tile_positionencoder_kernel(tc, state, W_words, W_scales, b, gamma, beta, out):
+    nc = tc.nc
+    with (
+        tc.tile_pool(name="const", bufs=1) as const,
+        tc.tile_pool(name="rows", bufs=4) as rows,
+        tc.tile_pool(name="scratch", bufs=2) as scratch,
+        tc.tile_pool(name="stats", bufs=4) as stats,
+        tc.psum_pool(name="psum", bufs=8) as psum,
+    ):
+        state_sb = const.tile([P, ROW_TILES * COORDS], BF16)
+        nc.sync.dma_start(out=state_sb[:], in_=state.rearrange("(m i) c -> m (i c)", i=ROW_TILES))
+
+        w_scales = const.tile([P, N_OUT], U8, align_bytes=64)
+        nc.vector.memset(w_scales[:].bitcast(I32), 0)
+        for low in range(2):
+            for r in range(4):
+                nc.sync.dma_start(
+                    out=w_scales[32 * low + r : P : 64, :].bitcast(I32),
+                    in_=W_scales[0, 4 * low + r : 16 : 8, :].bitcast(I32),
+                )
+
+        w_codes = const.tile([P, N_OUT], U32, align_bytes=64)
+        w_words = W_words[0].rearrange("p n t -> p (n t)").bitcast(I32)
+        for piece in range(4):
+            cols = slice(piece * 1024, (piece + 1) * 1024)
+            nc.sync.dma_start(out=w_codes[:, cols].bitcast(I32), in_=w_words[:, cols])
+
+        b_all = const.tile([P, N_OUT], BF16)
+        nc.scalar.dma_start(out=b_all[:], in_=b.partition_broadcast(P))
+        gamma_all = const.tile([P, N_OUT], BF16)
+        nc.scalar.dma_start(out=gamma_all[:], in_=gamma.partition_broadcast(P))
+        beta_all = const.tile([P, N_OUT], BF16)
+        nc.scalar.dma_start(out=beta_all[:], in_=beta.partition_broadcast(P))
+
+        k_index = const.tile([P, PACK], I32)
+        nc.gpsimd.iota(k_index[:], pattern=[[1, PACK]], base=0, channel_multiplier=PACK)
+        j_index = const.tile([P, PACK], I32)
+        nc.vector.tensor_single_scalar(
+            out=j_index[:], in_=k_index[:], scalar=PER_COORD - 1, op=ALU.bitwise_and
+        )
+        j_float = const.tile([P, PACK], F32)
+        nc.vector.tensor_copy(out=j_float[:], in_=j_index[:])
+        freq = const.tile([P, PACK], F32)
+        nc.scalar.activation(
+            out=freq[:], in_=j_float[:], func=ACT.Exp, scale=-2.0 * math.log(10000.0) / PER_COORD
+        )
+
+        identity = const.tile([P, P], F32)
+        make_identity(nc, identity[:])
+        s_low = const.tile([P, ROW_TILES * COORDS], F32)
+        nc.vector.tensor_scalar(
+            out=s_low[:], in0=state_sb[:], scalar1=1.0 / MAX_COORD, scalar2=0.0,
+            op0=ALU.mult, op1=ALU.max,
+        )
+        s_wide = const.tile([P, ROW_TILES * COORDS, P // COORDS], F32)
+        nc.vector.tensor_scalar_min(
+            out=s_wide[:],
+            in0=s_low[:].unsqueeze(2).to_broadcast([P, ROW_TILES * COORDS, P // COORDS]),
+            scalar1=1.0,
+        )
+
+        pe_planes = const.tile([P, PACK, ROWS], BF16)
+        pe_grouped = const.tile([P, ROWS, PACK], BF16, align_bytes=64)
+        pe_codes = const.tile([P, ROWS], U32, align_bytes=64)
+        pe_scales = const.tile([P, ROWS], U8, align_bytes=64)
+        for half in range(ROWS // BANK):
+            cols = slice(half * BANK, (half + 1) * BANK)
+            s_t = psum.tile([P, BANK], F32, tag="bank")
+            for q in range(BANK // P):
+                i = half * (BANK // P) + q
+                nc.tensor.transpose(
+                    s_t[:, q * P : (q + 1) * P],
+                    s_wide[:, i * COORDS : (i + 1) * COORDS, :].rearrange("m c e -> m (c e)"),
+                    identity[:],
+                )
+            for t in range(PACK):
+                if t % 2 == 0:
+                    nc.scalar.activation(
+                        out=pe_planes[:, t, cols], in_=s_t[:], func=ACT.Sin,
+                        scale=freq[:, t : t + 1],
+                    )
+                else:
+                    angle = scratch.tile([P, BANK], F32)
+                    nc.vector.tensor_scalar(
+                        out=angle[:], in0=s_t[:], scalar1=freq[:, t : t + 1],
+                        scalar2=math.pi / 2.0, op0=ALU.mult, op1=ALU.add,
+                    )
+                    nc.scalar.activation(out=pe_planes[:, t, cols], in_=angle[:], func=ACT.Sin)
+            nc.vector.tensor_copy(
+                out=pe_grouped[:, cols, :], in_=pe_planes[:, :, cols].rearrange("p t r -> p r t")
+            )
+            nc.vector.quantize_mx(
+                out=pe_codes[:, cols].bitcast(FP8X4),
+                scales=pe_scales[:, cols],
+                in_=pe_grouped[:, cols, :].rearrange("p r t -> p (r t)"),
+            )
+
+        out_tiles = out.rearrange("(m i) n -> m i n", i=ROW_TILES)
+        for i in range(ROW_TILES):
+            tile_rows = slice(i * P, (i + 1) * P)
+            y = rows.tile([P, N_OUT], F32)
+            y_sums = stats.tile([P, BANKS], F32)
+            for blk in range(BANKS):
+                cols = slice(blk * BANK, (blk + 1) * BANK)
+                acc = psum.tile([P, BANK], F32, tag="bank")
+                nc.tensor.matmul_mx(
+                    out=acc[:],
+                    lhsT=pe_codes[:, tile_rows].bitcast(FP8X4),
+                    lhsT_scale=pe_scales[:, tile_rows],
+                    rhs=w_codes[:, cols].bitcast(FP8X4),
+                    rhs_scale=w_scales[:, cols],
+                    start=True,
+                    stop=True,
+                )
+                nc.vector.scalar_tensor_tensor(
+                    out=y[:, cols], in0=acc[:], scalar=1.0, in1=b_all[:, cols],
+                    op0=ALU.mult, op1=ALU.add, accum_out=y_sums[:, blk : blk + 1],
+                )
+            y_sum = stats.tile([P, 1], F32)
+            nc.vector.tensor_reduce(out=y_sum[:], in_=y_sums[:], axis=AXIS.X, op=ALU.add)
+            neg_mean = stats.tile([P, 1], F32)
+            nc.vector.tensor_scalar_mul(out=neg_mean[:], in0=y_sum[:], scalar1=-1.0 / N_OUT)
+            squares = scratch.tile([P, N_OUT], BF16)
+            sum_sq = stats.tile([P, 1], F32)
+            nc.scalar.activation(
+                out=squares[:], in_=y[:], func=ACT.Square, bias=neg_mean[:, 0:1],
+                accum_out=sum_sq[:],
+            )
+            var_eps = stats.tile([P, 1], F32)
+            nc.vector.tensor_scalar(
+                out=var_eps[:], in0=sum_sq[:], scalar1=1.0 / N_OUT, scalar2=LN_EPS,
+                op0=ALU.mult, op1=ALU.add,
+            )
+            std = stats.tile([P, 1], F32)
+            nc.scalar.activation(out=std[:], in_=var_eps[:], func=ACT.Sqrt)
+            rstd = stats.tile([P, 1], F32)
+            nc.vector.reciprocal(out=rstd[:], in_=std[:])
+            for piece in range(2):
+                cols = slice(piece * (N_OUT // 2), (piece + 1) * (N_OUT // 2))
+                nc.vector.scalar_tensor_tensor(
+                    out=y[:, cols], in0=y[:, cols], scalar=neg_mean[:, 0:1],
+                    in1=gamma_all[:, cols], op0=ALU.add, op1=ALU.mult,
+                )
+                nc.vector.scalar_tensor_tensor(
+                    out=y[:, cols], in0=y[:, cols], scalar=rstd[:, 0:1],
+                    in1=beta_all[:, cols], op0=ALU.mult, op1=ALU.add,
+                )
+                nc.sync.dma_start(out=out_tiles[:, i, cols], in_=y[:, cols])

@@ -22,6 +22,7 @@ N_OUT = 4096
 BANK = 512
 ROW_TILES = ROWS // P
 BANKS = N_OUT // BANK
+GAIN_BANK = 1024
 MAX_COORD = 10.0
 LN_EPS = 1e-5
 
@@ -32,10 +33,11 @@ def tile_positionencoder_kernel(tc, state, W_words, W_scales, b, gamma, beta, ou
     nc = tc.nc
     with (
         tc.tile_pool(name="const", bufs=1) as const,
-        tc.tile_pool(name="rows", bufs=4) as rows,
+        tc.tile_pool(name="rows", bufs=6) as rows,
         tc.tile_pool(name="scratch", bufs=2) as scratch,
         tc.tile_pool(name="stats", bufs=4) as stats,
-        tc.psum_pool(name="psum", bufs=8) as psum,
+        tc.psum_pool(name="gain", bufs=1) as gain,
+        tc.psum_pool(name="psum", bufs=4) as psum,
     ):
         state_sb = const.tile([P, ROW_TILES * COORDS], BF16)
         nc.sync.dma_start(out=state_sb[:], in_=state.rearrange("(m i) c -> m (i c)", i=ROW_TILES))
@@ -57,8 +59,9 @@ def tile_positionencoder_kernel(tc, state, W_words, W_scales, b, gamma, beta, ou
 
         b_all = const.tile([P, N_OUT], BF16)
         nc.scalar.dma_start(out=b_all[:], in_=b.partition_broadcast(P))
-        gamma_all = const.tile([P, N_OUT], BF16)
-        nc.scalar.dma_start(out=gamma_all[:], in_=gamma.partition_broadcast(P))
+        gamma_row = const.tile([P, N_OUT], BF16)
+        nc.vector.memset(gamma_row[:].bitcast(I32), 0)
+        nc.scalar.dma_start(out=gamma_row[0:1, :], in_=gamma.unsqueeze(0))
         beta_all = const.tile([P, N_OUT], BF16)
         nc.scalar.dma_start(out=beta_all[:], in_=beta.partition_broadcast(P))
 
@@ -125,6 +128,19 @@ def tile_positionencoder_kernel(tc, state, W_words, W_scales, b, gamma, beta, ou
                 in_=pe_grouped[:, cols, :].rearrange("p r t -> p (r t)"),
             )
 
+        ones = const.tile([P, P], BF16)
+        nc.vector.memset(ones[:], 1.0)
+        gamma_banks = []
+        for g in range(N_OUT // GAIN_BANK):
+            gamma_bank = gain.tile([P, GAIN_BANK], BF16, name="gamma_bank%d" % g)
+            for h in range(GAIN_BANK // BANK):
+                cols = slice(g * GAIN_BANK + h * BANK, g * GAIN_BANK + (h + 1) * BANK)
+                nc.tensor.matmul(
+                    out=gamma_bank[:, h * BANK : (h + 1) * BANK], lhsT=ones[:],
+                    rhs=gamma_row[:, cols], start=True, stop=True,
+                )
+            gamma_banks.append(gamma_bank)
+
         out_tiles = out.rearrange("(m i) n -> m i n", i=ROW_TILES)
         for i in range(ROW_TILES):
             tile_rows = slice(i * P, (i + 1) * P)
@@ -165,14 +181,14 @@ def tile_positionencoder_kernel(tc, state, W_words, W_scales, b, gamma, beta, ou
             nc.scalar.activation(out=std[:], in_=var_eps[:], func=ACT.Sqrt)
             rstd = stats.tile([P, 1], F32)
             nc.vector.reciprocal(out=rstd[:], in_=std[:])
-            for piece in range(2):
-                cols = slice(piece * (N_OUT // 2), (piece + 1) * (N_OUT // 2))
-                nc.vector.scalar_tensor_tensor(
-                    out=y[:, cols], in0=y[:, cols], scalar=neg_mean[:, 0:1],
-                    in1=gamma_all[:, cols], op0=ALU.add, op1=ALU.mult,
+            shift = stats.tile([P, 1], F32)
+            nc.vector.tensor_mul(out=shift[:], in0=neg_mean[:], in1=rstd[:])
+            for g in range(N_OUT // GAIN_BANK):
+                cols = slice(g * GAIN_BANK, (g + 1) * GAIN_BANK)
+                nc.scalar.activation(
+                    out=y[:, cols], in_=y[:, cols], func=ACT.Identity,
+                    scale=rstd[:, 0:1], bias=shift[:, 0:1],
                 )
-                nc.vector.scalar_tensor_tensor(
-                    out=y[:, cols], in0=y[:, cols], scalar=rstd[:, 0:1],
-                    in1=beta_all[:, cols], op0=ALU.mult, op1=ALU.add,
-                )
+                nc.vector.tensor_mul(out=y[:, cols], in0=y[:, cols], in1=gamma_banks[g][:])
+                nc.gpsimd.tensor_add(out=y[:, cols], in0=y[:, cols], in1=beta_all[:, cols])
                 nc.sync.dma_start(out=out_tiles[:, i, cols], in_=y[:, cols])

@@ -23,6 +23,9 @@ BANK = 512
 ROW_TILES = ROWS // P
 BANKS = N_OUT // BANK
 GAIN_BANK = 1024
+GROUPS = N_OUT // GAIN_BANK
+GPSIMD_GROUPS = 3
+PIECE = 256
 MAX_COORD = 10.0
 LN_EPS = 1e-5
 
@@ -33,8 +36,10 @@ def tile_positionencoder_kernel(tc, state, W_words, W_scales, b, gamma, beta, ou
     nc = tc.nc
     with (
         tc.tile_pool(name="const", bufs=1) as const,
-        tc.tile_pool(name="rows", bufs=6) as rows,
+        tc.tile_pool(name="rows", bufs=3) as rows,
+        tc.tile_pool(name="results", bufs=4) as results,
         tc.tile_pool(name="scratch", bufs=2) as scratch,
+        tc.tile_pool(name="angles", bufs=8) as angles,
         tc.tile_pool(name="stats", bufs=4) as stats,
         tc.psum_pool(name="gain", bufs=1) as gain,
         tc.psum_pool(name="psum", bufs=4) as psum,
@@ -57,16 +62,20 @@ def tile_positionencoder_kernel(tc, state, W_words, W_scales, b, gamma, beta, ou
             cols = slice(piece * 1024, (piece + 1) * 1024)
             nc.sync.dma_start(out=w_codes[:, cols].bitcast(I32), in_=w_words[:, cols])
 
-        b_all = const.tile([P, N_OUT], BF16)
-        nc.scalar.dma_start(out=b_all[:], in_=b.partition_broadcast(P))
         gamma_row = const.tile([P, N_OUT], BF16)
         nc.vector.memset(gamma_row[:].bitcast(I32), 0)
         nc.scalar.dma_start(out=gamma_row[0:1, :], in_=gamma.unsqueeze(0))
+        b_all = const.tile([P, N_OUT], BF16)
+        nc.scalar.dma_start(out=b_all[:], in_=b.partition_broadcast(P))
         beta_all = const.tile([P, N_OUT], BF16)
         nc.scalar.dma_start(out=beta_all[:], in_=beta.partition_broadcast(P))
+        ones = const.tile([P, P], BF16)
+        nc.vector.memset(ones[:], 1.0)
 
         k_index = const.tile([P, PACK], I32)
         nc.gpsimd.iota(k_index[:], pattern=[[1, PACK]], base=0, channel_multiplier=PACK)
+        identity = const.tile([P, P], F32)
+        make_identity(nc, identity[:])
         j_index = const.tile([P, PACK], I32)
         nc.vector.tensor_single_scalar(
             out=j_index[:], in_=k_index[:], scalar=PER_COORD - 1, op=ALU.bitwise_and
@@ -78,8 +87,6 @@ def tile_positionencoder_kernel(tc, state, W_words, W_scales, b, gamma, beta, ou
             out=freq[:], in_=j_float[:], func=ACT.Exp, scale=-2.0 * math.log(10000.0) / PER_COORD
         )
 
-        identity = const.tile([P, P], F32)
-        make_identity(nc, identity[:])
         s_low = const.tile([P, ROW_TILES * COORDS], F32)
         nc.vector.tensor_scalar(
             out=s_low[:], in0=state_sb[:], scalar1=1.0 / MAX_COORD, scalar2=0.0,
@@ -96,11 +103,11 @@ def tile_positionencoder_kernel(tc, state, W_words, W_scales, b, gamma, beta, ou
         pe_grouped = const.tile([P, ROWS, PACK], BF16, align_bytes=64)
         pe_codes = const.tile([P, ROWS], U32, align_bytes=64)
         pe_scales = const.tile([P, ROWS], U8, align_bytes=64)
-        for half in range(ROWS // BANK):
-            cols = slice(half * BANK, (half + 1) * BANK)
-            s_t = psum.tile([P, BANK], F32, tag="bank")
-            for q in range(BANK // P):
-                i = half * (BANK // P) + q
+        pieces = [slice(piece * PIECE, (piece + 1) * PIECE) for piece in range(ROWS // PIECE)]
+        for piece, cols in enumerate(pieces):
+            s_t = psum.tile([P, PIECE], F32, tag="bank")
+            for q in range(PIECE // P):
+                i = piece * (PIECE // P) + q
                 nc.tensor.transpose(
                     s_t[:, q * P : (q + 1) * P],
                     s_wide[:, i * COORDS : (i + 1) * COORDS, :].rearrange("m c e -> m (c e)"),
@@ -113,12 +120,14 @@ def tile_positionencoder_kernel(tc, state, W_words, W_scales, b, gamma, beta, ou
                         scale=freq[:, t : t + 1],
                     )
                 else:
-                    angle = scratch.tile([P, BANK], F32)
+                    angle = angles.tile([P, PIECE], F32)
                     nc.vector.tensor_scalar(
                         out=angle[:], in0=s_t[:], scalar1=freq[:, t : t + 1],
                         scalar2=math.pi / 2.0, op0=ALU.mult, op1=ALU.add,
                     )
                     nc.scalar.activation(out=pe_planes[:, t, cols], in_=angle[:], func=ACT.Sin)
+
+        def quantise(cols):
             nc.vector.tensor_copy(
                 out=pe_grouped[:, cols, :], in_=pe_planes[:, :, cols].rearrange("p t r -> p r t")
             )
@@ -128,10 +137,10 @@ def tile_positionencoder_kernel(tc, state, W_words, W_scales, b, gamma, beta, ou
                 in_=pe_grouped[:, cols, :].rearrange("p r t -> p (r t)"),
             )
 
-        ones = const.tile([P, P], BF16)
-        nc.vector.memset(ones[:], 1.0)
+        quantise(pieces[0])
+
         gamma_banks = []
-        for g in range(N_OUT // GAIN_BANK):
+        for g in range(GROUPS):
             gamma_bank = gain.tile([P, GAIN_BANK], BF16, name="gamma_bank%d" % g)
             for h in range(GAIN_BANK // BANK):
                 cols = slice(g * GAIN_BANK + h * BANK, g * GAIN_BANK + (h + 1) * BANK)
@@ -142,13 +151,15 @@ def tile_positionencoder_kernel(tc, state, W_words, W_scales, b, gamma, beta, ou
             gamma_banks.append(gamma_bank)
 
         out_tiles = out.rearrange("(m i) n -> m i n", i=ROW_TILES)
-        for i in range(ROW_TILES):
+        groups = [slice(g * GAIN_BANK, (g + 1) * GAIN_BANK) for g in range(GROUPS)]
+
+        def product(i):
             tile_rows = slice(i * P, (i + 1) * P)
-            y = rows.tile([P, N_OUT], F32)
-            y_sums = stats.tile([P, BANKS], F32)
+            y = rows.tile([P, N_OUT], F32, name="y")
+            y_sums = stats.tile([P, BANKS], F32, name="y_sums")
             for blk in range(BANKS):
                 cols = slice(blk * BANK, (blk + 1) * BANK)
-                acc = psum.tile([P, BANK], F32, tag="bank")
+                acc = psum.tile([P, BANK], F32, tag="bank", name="acc")
                 nc.tensor.matmul_mx(
                     out=acc[:],
                     lhsT=pe_codes[:, tile_rows].bitcast(FP8X4),
@@ -162,33 +173,57 @@ def tile_positionencoder_kernel(tc, state, W_words, W_scales, b, gamma, beta, ou
                     out=y[:, cols], in0=acc[:], scalar=1.0, in1=b_all[:, cols],
                     op0=ALU.mult, op1=ALU.add, accum_out=y_sums[:, blk : blk + 1],
                 )
-            y_sum = stats.tile([P, 1], F32)
+            y_sum = stats.tile([P, 1], F32, name="y_sum")
             nc.vector.tensor_reduce(out=y_sum[:], in_=y_sums[:], axis=AXIS.X, op=ALU.add)
-            neg_mean = stats.tile([P, 1], F32)
+            neg_mean = stats.tile([P, 1], F32, name="neg_mean")
             nc.vector.tensor_scalar_mul(out=neg_mean[:], in0=y_sum[:], scalar1=-1.0 / N_OUT)
-            squares = scratch.tile([P, N_OUT], BF16)
-            sum_sq = stats.tile([P, 1], F32)
-            nc.scalar.activation(
-                out=squares[:], in_=y[:], func=ACT.Square, bias=neg_mean[:, 0:1],
-                accum_out=sum_sq[:],
-            )
-            var_eps = stats.tile([P, 1], F32)
-            nc.vector.tensor_scalar(
-                out=var_eps[:], in0=sum_sq[:], scalar1=1.0 / N_OUT, scalar2=LN_EPS,
-                op0=ALU.mult, op1=ALU.add,
-            )
-            std = stats.tile([P, 1], F32)
-            nc.scalar.activation(out=std[:], in_=var_eps[:], func=ACT.Sqrt)
-            rstd = stats.tile([P, 1], F32)
-            nc.vector.reciprocal(out=rstd[:], in_=std[:])
-            shift = stats.tile([P, 1], F32)
-            nc.vector.tensor_mul(out=shift[:], in0=neg_mean[:], in1=rstd[:])
-            for g in range(N_OUT // GAIN_BANK):
-                cols = slice(g * GAIN_BANK, (g + 1) * GAIN_BANK)
+            return y, neg_mean
+
+        def finish(i, result, rstd):
+            for g, cols in enumerate(groups):
+                if g >= GPSIMD_GROUPS or i == ROW_TILES - 1:
+                    nc.vector.scalar_tensor_tensor(
+                        out=result[:, cols], in0=result[:, cols], scalar=rstd[:, 0:1],
+                        in1=beta_all[:, cols], op0=ALU.mult, op1=ALU.add,
+                    )
+                else:
+                    nc.scalar.mul(out=result[:, cols], in_=result[:, cols], mul=rstd[:, 0:1])
+                    nc.gpsimd.tensor_add(
+                        out=result[:, cols], in0=result[:, cols], in1=beta_all[:, cols]
+                    )
+                nc.sync.dma_start(out=out_tiles[:, i, cols], in_=result[:, cols])
+
+        y, neg_mean = product(0)
+        for cols in pieces[1:]:
+            quantise(cols)
+        earlier = None
+        for i in range(ROW_TILES + 1):
+            if i < ROW_TILES:
+                squares = scratch.tile([P, N_OUT], BF16)
+                sum_sq = stats.tile([P, 1], F32)
                 nc.scalar.activation(
-                    out=y[:, cols], in_=y[:, cols], func=ACT.Identity,
-                    scale=rstd[:, 0:1], bias=shift[:, 0:1],
+                    out=squares[:], in_=y[:], func=ACT.Square, bias=neg_mean[:, 0:1],
+                    accum_out=sum_sq[:],
                 )
-                nc.vector.tensor_mul(out=y[:, cols], in0=y[:, cols], in1=gamma_banks[g][:])
-                nc.gpsimd.tensor_add(out=y[:, cols], in0=y[:, cols], in1=beta_all[:, cols])
-                nc.sync.dma_start(out=out_tiles[:, i, cols], in_=y[:, cols])
+                result = results.tile([P, N_OUT], F32)
+                for g, cols in enumerate(groups):
+                    nc.vector.scalar_tensor_tensor(
+                        out=result[:, cols], in0=y[:, cols], scalar=neg_mean[:, 0:1],
+                        in1=gamma_banks[g][:], op0=ALU.add, op1=ALU.mult,
+                    )
+            if earlier is not None:
+                rstd = stats.tile([P, 1], F32)
+                nc.vector.reciprocal(out=rstd[:], in_=earlier[1][:])
+            if i + 1 < ROW_TILES:
+                y, neg_mean = product(i + 1)
+            if earlier is not None:
+                finish(i - 1, earlier[0], rstd)
+            if i < ROW_TILES:
+                var_eps = stats.tile([P, 1], F32)
+                nc.vector.tensor_scalar(
+                    out=var_eps[:], in0=sum_sq[:], scalar1=1.0 / N_OUT, scalar2=LN_EPS,
+                    op0=ALU.mult, op1=ALU.add,
+                )
+                std = stats.tile([P, 1], F32)
+                nc.scalar.activation(out=std[:], in_=var_eps[:], func=ACT.Sqrt)
+                earlier = (result, std)

@@ -24,7 +24,7 @@ ROW_TILES = ROWS // P
 BANKS = N_OUT // BANK
 GAIN_BANK = 1024
 GROUPS = N_OUT // GAIN_BANK
-GPSIMD_GROUPS = 3
+GPSIMD_GROUPS = 4
 PIECE = 256
 MAX_COORD = 10.0
 LN_EPS = 1e-5

@@ -24,8 +24,12 @@ ROW_TILES = ROWS // P
 BANKS = N_OUT // BANK
 GAIN_BANK = 1024
 GROUPS = N_OUT // GAIN_BANK
-GPSIMD_GROUPS = 4
-PIECE = 256
+PIECES = (slice(0, 128), slice(128, 384), slice(384, 640), slice(640, 896), slice(896, 1024))
+FLIPPED_ROWS = PIECES[1]
+FLIPPED_TILES = (1, 2)
+FLIPPED_WIDTH = len(FLIPPED_TILES) * P
+OUT_BLOCKS = N_OUT // P
+PARTS = 3
 MAX_COORD = 10.0
 LN_EPS = 1e-5
 
@@ -36,25 +40,29 @@ def tile_positionencoder_kernel(tc, state, W_words, W_scales, b, gamma, beta, ou
     nc = tc.nc
     with (
         tc.tile_pool(name="const", bufs=1) as const,
-        tc.tile_pool(name="rows", bufs=3) as rows,
-        tc.tile_pool(name="results", bufs=4) as results,
+        tc.tile_pool(name="rows", bufs=4) as rows,
         tc.tile_pool(name="scratch", bufs=2) as scratch,
-        tc.tile_pool(name="angles", bufs=8) as angles,
         tc.tile_pool(name="stats", bufs=4) as stats,
         tc.psum_pool(name="gain", bufs=1) as gain,
-        tc.psum_pool(name="psum", bufs=4) as psum,
+        tc.psum_pool(name="psum", bufs=2) as psum,
+        tc.psum_pool(name="side", bufs=2) as side,
     ):
         state_sb = const.tile([P, ROW_TILES * COORDS], BF16)
         nc.sync.dma_start(out=state_sb[:], in_=state.rearrange("(m i) c -> m (i c)", i=ROW_TILES))
 
+        by_block = const.tile([P, P], BF16)
+        nc.vector.memset(by_block[:].bitcast(I32), 0)
+        nc.sync.dma_start(out=by_block[0:OUT_BLOCKS, :], in_=b.rearrange("(j p) -> j p", p=P))
+        nc.sync.dma_start(
+            out=by_block[OUT_BLOCKS : 2 * OUT_BLOCKS, :], in_=gamma.rearrange("(j p) -> j p", p=P)
+        )
+
         w_scales = const.tile([P, N_OUT], U8, align_bytes=64)
         nc.vector.memset(w_scales[:].bitcast(I32), 0)
-        for low in range(2):
-            for r in range(4):
-                nc.sync.dma_start(
-                    out=w_scales[32 * low + r : P : 64, :].bitcast(I32),
-                    in_=W_scales[0, 4 * low + r : 16 : 8, :].bitcast(I32),
-                )
+        for r in range(4):
+            nc.sync.dma_start(
+                out=w_scales[r:P:32, :].bitcast(I32), in_=W_scales[0, r:16:4, :].bitcast(I32)
+            )
 
         w_codes = const.tile([P, N_OUT], U32, align_bytes=64)
         w_words = W_words[0].rearrange("p n t -> p (n t)").bitcast(I32)
@@ -62,15 +70,10 @@ def tile_positionencoder_kernel(tc, state, W_words, W_scales, b, gamma, beta, ou
             cols = slice(piece * 1024, (piece + 1) * 1024)
             nc.sync.dma_start(out=w_codes[:, cols].bitcast(I32), in_=w_words[:, cols])
 
-        gamma_row = const.tile([P, N_OUT], BF16)
-        nc.vector.memset(gamma_row[:].bitcast(I32), 0)
-        nc.scalar.dma_start(out=gamma_row[0:1, :], in_=gamma.unsqueeze(0))
         b_all = const.tile([P, N_OUT], BF16)
-        nc.scalar.dma_start(out=b_all[:], in_=b.partition_broadcast(P))
+        nc.sync.dma_start(out=b_all[:], in_=b.partition_broadcast(P))
         beta_all = const.tile([P, N_OUT], BF16)
-        nc.scalar.dma_start(out=beta_all[:], in_=beta.partition_broadcast(P))
-        ones = const.tile([P, P], BF16)
-        nc.vector.memset(ones[:], 1.0)
+        nc.sync.dma_start(out=beta_all[:], in_=beta.partition_broadcast(P))
 
         k_index = const.tile([P, PACK], I32)
         nc.gpsimd.iota(k_index[:], pattern=[[1, PACK]], base=0, channel_multiplier=PACK)
@@ -80,12 +83,23 @@ def tile_positionencoder_kernel(tc, state, W_words, W_scales, b, gamma, beta, ou
         nc.vector.tensor_single_scalar(
             out=j_index[:], in_=k_index[:], scalar=PER_COORD - 1, op=ALU.bitwise_and
         )
-        j_float = const.tile([P, PACK], F32)
-        nc.vector.tensor_copy(out=j_float[:], in_=j_index[:])
+        exponent = const.tile([P, PACK], F32)
+        nc.vector.tensor_scalar_mul(out=exponent[:], in0=j_index[:], scalar1=-2.0 / PER_COORD)
+        base = const.tile([P, PACK], F32)
+        nc.gpsimd.memset(base[:], 10000.0)
         freq = const.tile([P, PACK], F32)
-        nc.scalar.activation(
-            out=freq[:], in_=j_float[:], func=ACT.Exp, scale=-2.0 * math.log(10000.0) / PER_COORD
+        nc.gpsimd.tensor_tensor(out=freq[:], in0=base[:], in1=exponent[:], op=ALU.pow)
+        half_pi = const.tile([P, 1], F32)
+        nc.vector.tensor_scalar(
+            out=half_pi[:], in0=base[:, 0:1], scalar1=0.0, scalar2=math.pi / 2.0,
+            op0=ALU.mult, op1=ALU.add,
         )
+        eps = const.tile([P, 1], F32)
+        nc.vector.tensor_scalar(
+            out=eps[:], in0=base[:, 0:1], scalar1=0.0, scalar2=LN_EPS, op0=ALU.mult, op1=ALU.add
+        )
+        warm = const.tile([P, 1], F32)
+        nc.scalar.activation(out=warm[:], in_=half_pi[:], func=ACT.Sin)
 
         s_low = const.tile([P, ROW_TILES * COORDS], F32)
         nc.vector.tensor_scalar(
@@ -99,33 +113,37 @@ def tile_positionencoder_kernel(tc, state, W_words, W_scales, b, gamma, beta, ou
             scalar1=1.0,
         )
 
+        identity_bf16 = const.tile([P, P], BF16)
+        nc.vector.tensor_copy(out=identity_bf16[:], in_=identity[:])
+        ones = const.tile([P, P], BF16)
+        nc.vector.memset(ones[:], 1.0)
+        vectors = const.tile([P, N_OUT], BF16)
+        nc.gpsimd.memset(vectors[:].bitcast(I32), 0)
+        nc.sync.dma_start(out=vectors[0:PARTS, :], in_=gamma.partition_broadcast(PARTS))
+        nc.sync.dma_start(out=vectors[PARTS : 2 * PARTS, :], in_=beta.partition_broadcast(PARTS))
+        split = const.tile([P, len(FLIPPED_TILES), P], BF16)
+        nc.gpsimd.memset(split[:].bitcast(I32), 0)
+
         pe_planes = const.tile([P, PACK, ROWS], BF16)
         pe_grouped = const.tile([P, ROWS, PACK], BF16, align_bytes=64)
         pe_codes = const.tile([P, ROWS], U32, align_bytes=64)
         pe_scales = const.tile([P, ROWS], U8, align_bytes=64)
-        pieces = [slice(piece * PIECE, (piece + 1) * PIECE) for piece in range(ROWS // PIECE)]
-        for piece, cols in enumerate(pieces):
-            s_t = psum.tile([P, PIECE], F32, tag="bank")
-            for q in range(PIECE // P):
-                i = piece * (PIECE // P) + q
+
+        def encode(cols):
+            count = cols.stop - cols.start
+            s_t = psum.tile([P, count], F32, tag="bank", name="s_t")
+            for q in range(count // P):
+                i = cols.start // P + q
                 nc.tensor.transpose(
                     s_t[:, q * P : (q + 1) * P],
                     s_wide[:, i * COORDS : (i + 1) * COORDS, :].rearrange("m c e -> m (c e)"),
                     identity[:],
                 )
             for t in range(PACK):
-                if t % 2 == 0:
-                    nc.scalar.activation(
-                        out=pe_planes[:, t, cols], in_=s_t[:], func=ACT.Sin,
-                        scale=freq[:, t : t + 1],
-                    )
-                else:
-                    angle = angles.tile([P, PIECE], F32)
-                    nc.vector.tensor_scalar(
-                        out=angle[:], in0=s_t[:], scalar1=freq[:, t : t + 1],
-                        scalar2=math.pi / 2.0, op0=ALU.mult, op1=ALU.add,
-                    )
-                    nc.scalar.activation(out=pe_planes[:, t, cols], in_=angle[:], func=ACT.Sin)
+                nc.scalar.activation(
+                    out=pe_planes[:, t, cols], in_=s_t[:], func=ACT.Sin,
+                    scale=freq[:, t : t + 1], bias=half_pi[:, 0:1] if t % 2 else 0.0,
+                )
 
         def quantise(cols):
             nc.vector.tensor_copy(
@@ -137,93 +155,253 @@ def tile_positionencoder_kernel(tc, state, W_words, W_scales, b, gamma, beta, ou
                 in_=pe_grouped[:, cols, :].rearrange("p r t -> p (r t)"),
             )
 
-        quantise(pieces[0])
+        encode(PIECES[0])
+        quantise(PIECES[0])
 
-        gamma_banks = []
-        for g in range(GROUPS):
-            gamma_bank = gain.tile([P, GAIN_BANK], BF16, name="gamma_bank%d" % g)
-            for h in range(GAIN_BANK // BANK):
-                cols = slice(g * GAIN_BANK + h * BANK, g * GAIN_BANK + (h + 1) * BANK)
-                nc.tensor.matmul(
-                    out=gamma_bank[:, h * BANK : (h + 1) * BANK], lhsT=ones[:],
-                    rhs=gamma_row[:, cols], start=True, stop=True,
+        cols_t = side.tile([P, P], BF16, tag="side", name="cols_t")
+        nc.tensor.transpose(cols_t[:], by_block[:], identity_bf16[:])
+        b_bf16 = const.tile([P, OUT_BLOCKS], BF16)
+        nc.vector.tensor_copy(out=b_bf16[:], in_=cols_t[:, :OUT_BLOCKS])
+        b_cols = const.tile([P, OUT_BLOCKS], F32)
+        nc.vector.tensor_copy(out=b_cols[:], in_=cols_t[:, :OUT_BLOCKS])
+        gamma_bf16 = const.tile([P, OUT_BLOCKS], BF16)
+        nc.vector.tensor_copy(out=gamma_bf16[:], in_=cols_t[:, OUT_BLOCKS : 2 * OUT_BLOCKS])
+        gamma_cols = const.tile([P, OUT_BLOCKS], F32)
+        nc.vector.tensor_copy(out=gamma_cols[:], in_=cols_t[:, OUT_BLOCKS : 2 * OUT_BLOCKS])
+        b_gamma_cols = const.tile([P, OUT_BLOCKS], F32)
+        nc.vector.tensor_mul(out=b_gamma_cols[:], in0=b_cols[:], in1=gamma_cols[:])
+        b_sums = side.tile([P, OUT_BLOCKS], F32, tag="side", name="b_sums")
+        nc.tensor.matmul(out=b_sums[:], lhsT=ones[:], rhs=b_bf16[:], start=True, stop=True)
+        neg_b_share = const.tile([P, 1], F32)
+        b_ignored = const.tile([P, OUT_BLOCKS], F32)
+        nc.scalar.activation(
+            out=b_ignored[:], in_=b_sums[:], func=ACT.Copy, scale=-1.0 / (N_OUT * BANK),
+            accum_out=neg_b_share[:],
+        )
+        neg_b_mean = const.tile([P, 1], F32)
+        nc.vector.tensor_scalar_mul(out=neg_b_mean[:], in0=neg_b_share[:], scalar1=float(BANK))
+        b_centred_cols = const.tile([P, OUT_BLOCKS], F32)
+        nc.vector.tensor_scalar_add(
+            out=b_centred_cols[:], in0=b_cols[:], scalar1=neg_b_mean[:, 0:1]
+        )
+
+        gamma_banks = [
+            gain.tile([P, GAIN_BANK], BF16, name="gamma_bank%d" % g) for g in range(GROUPS)
+        ]
+
+        def spread_gamma():
+            for j in range(OUT_BLOCKS):
+                g, h = divmod(j, GAIN_BANK // P)
+                nc.tensor.transpose(
+                    gamma_banks[g][:, h * P : (h + 1) * P],
+                    gamma_bf16[:, j : j + 1].to_broadcast([P, P]),
+                    identity_bf16[:],
                 )
-            gamma_banks.append(gamma_bank)
 
         out_tiles = out.rearrange("(m i) n -> m i n", i=ROW_TILES)
         groups = [slice(g * GAIN_BANK, (g + 1) * GAIN_BANK) for g in range(GROUPS)]
 
-        def product(i):
+        def multiply(acc, i, blk, start, stop):
             tile_rows = slice(i * P, (i + 1) * P)
-            y = rows.tile([P, N_OUT], F32, name="y")
-            y_sums = stats.tile([P, BANKS], F32, name="y_sums")
+            cols = slice(blk * BANK, (blk + 1) * BANK)
+            nc.tensor.matmul_mx(
+                out=acc[:],
+                lhsT=pe_codes[:, tile_rows].bitcast(FP8X4),
+                lhsT_scale=pe_scales[:, tile_rows],
+                rhs=w_codes[:, cols].bitcast(FP8X4),
+                rhs_scale=w_scales[:, cols],
+                start=start,
+                stop=stop,
+            )
+
+        def minus_mean(i, neg_mean, share):
+            total = side.tile([P, BANK], F32, tag="side", name="total")
+            for blk in range(BANKS):
+                multiply(total, i, blk, blk == 0, blk == BANKS - 1)
+            ignored = scratch.tile([P, BANK], BF16, name="ignored")
+            nc.scalar.activation(
+                out=ignored[:], in_=total[:], func=ACT.Identity, scale=-1.0 / N_OUT,
+                bias=share, accum_out=neg_mean,
+            )
+
+        scaled = const.tile([P, OUT_BLOCKS, FLIPPED_WIDTH], F32)
+        squared = const.tile([P, OUT_BLOCKS, FLIPPED_WIDTH], F32)
+
+        def flipped_products(pairs):
+            for pair in pairs:
+                acc = side.tile([P, 2, FLIPPED_WIDTH], F32, tag="side", name="flipped_acc")
+                for h in range(2):
+                    j = 2 * pair + h
+                    cols = slice(j * P, (j + 1) * P)
+                    nc.tensor.matmul_mx(
+                        out=acc[:, h, :],
+                        lhsT=w_codes[:, cols].bitcast(FP8X4),
+                        lhsT_scale=w_scales[:, cols],
+                        rhs=pe_codes[:, FLIPPED_ROWS].bitcast(FP8X4),
+                        rhs_scale=pe_scales[:, FLIPPED_ROWS],
+                        start=True,
+                        stop=True,
+                    )
+                for h in range(2):
+                    j = 2 * pair + h
+                    nc.scalar.activation(
+                        out=squared[:, j, :], in_=acc[:, h, :], func=ACT.Square,
+                        bias=b_centred_cols[:, j : j + 1],
+                    )
+                    nc.scalar.activation(
+                        out=scaled[:, j, :], in_=acc[:, h, :], func=ACT.Identity,
+                        scale=gamma_cols[:, j : j + 1], bias=b_gamma_cols[:, j : j + 1],
+                    )
+
+        neg_p_mean = const.tile([P, len(FLIPPED_TILES)], F32)
+        flipped_rstd = const.tile([P, len(FLIPPED_TILES)], F32)
+
+        def flipped_stats():
+            mean_sq = const.tile([P, len(FLIPPED_TILES)], F32)
+            for q in range(len(FLIPPED_TILES)):
+                sums = side.tile([P, P], F32, tag="side", name="sums")
+                for j in range(OUT_BLOCKS):
+                    nc.tensor.matmul(
+                        out=sums[:], lhsT=squared[:, j, q * P : (q + 1) * P], rhs=identity[:],
+                        is_transpose=True, start=(j == 0), stop=(j == OUT_BLOCKS - 1),
+                    )
+                ignored = scratch.tile([P, BANK], BF16, name="ignored")
+                nc.scalar.activation(
+                    out=ignored[:, :P], in_=sums[:], func=ACT.Copy, scale=1.0 / N_OUT,
+                    accum_out=mean_sq[:, q : q + 1],
+                )
+            mean_p_sq = const.tile([P, len(FLIPPED_TILES)], F32)
+            nc.vector.tensor_mul(out=mean_p_sq[:], in0=neg_p_mean[:], in1=neg_p_mean[:])
+            var_eps = const.tile([P, len(FLIPPED_TILES)], F32)
+            nc.vector.scalar_tensor_tensor(
+                out=var_eps[:], in0=mean_sq[:], scalar=LN_EPS, in1=mean_p_sq[:],
+                op0=ALU.add, op1=ALU.subtract,
+            )
+            nc.scalar.activation(
+                out=flipped_rstd[:], in_=var_eps[:], func=ACT.Abs_reciprocal_sqrt
+            )
+            rest = const.tile([P, len(FLIPPED_TILES), 2], F32)
+            nc.vector.tensor_scalar_add(
+                out=rest[:, :, 0], in0=neg_p_mean[:], scalar1=neg_b_mean[:, 0:1]
+            )
+            nc.vector.tensor_mul(out=rest[:, :, 1], in0=var_eps[:], in1=flipped_rstd[:])
+            parts = split[:, :, : 2 * PARTS].rearrange("m q (v s) -> m q v s", s=PARTS)
+            for s in range(PARTS):
+                nc.vector.tensor_copy(out=parts[:, :, :, s], in_=rest[:])
+                if s + 1 < PARTS:
+                    nc.vector.tensor_sub(out=rest[:], in0=rest[:], in1=parts[:, :, :, s])
+            split_t = const.tile([P, len(FLIPPED_TILES), P], BF16)
+            for q in range(len(FLIPPED_TILES)):
+                turned = side.tile([P, P], BF16, tag="side", name="turned")
+                nc.tensor.transpose(turned[:], split[:, q, :], identity_bf16[:])
+                nc.scalar.copy(out=split_t[:, q, :], in_=turned[:])
+            return split_t
+
+        def flipped_finish(split_t, tiles):
+            for q in tiles:
+                i = FLIPPED_TILES[q]
+                result = rows.tile([P, N_OUT], F32, tag="y", name="result")
+                for blk in range(BANKS):
+                    cols = slice(blk * BANK, (blk + 1) * BANK)
+                    acc = side.tile([P, BANK], F32, tag="side", name="turned_acc")
+                    nc.tensor.matmul(
+                        out=acc[:], lhsT=split_t[:, q, :], rhs=vectors[:, cols],
+                        start=True, stop=False,
+                    )
+                    for h in range(BANK // P):
+                        nc.tensor.matmul(
+                            out=acc[:, h * P : (h + 1) * P],
+                            lhsT=scaled[:, blk * (BANK // P) + h, q * P : (q + 1) * P],
+                            rhs=identity[:], is_transpose=True, start=False,
+                            stop=(h == BANK // P - 1),
+                        )
+                    if blk % 2 == 0 or q == 0:
+                        nc.scalar.mul(
+                            out=result[:, cols], in_=acc[:], mul=flipped_rstd[:, q : q + 1]
+                        )
+                    else:
+                        nc.vector.tensor_scalar_mul(
+                            out=result[:, cols], in0=acc[:], scalar1=flipped_rstd[:, q : q + 1]
+                        )
+                    if blk % 2 == 1:
+                        stored = slice((blk - 1) * BANK, (blk + 1) * BANK)
+                        nc.sync.dma_start(out=out_tiles[:, i, stored], in_=result[:, stored])
+
+        def centred(i, neg_mean):
+            y = rows.tile([P, N_OUT], F32, tag="y", name="y")
             for blk in range(BANKS):
                 cols = slice(blk * BANK, (blk + 1) * BANK)
                 acc = psum.tile([P, BANK], F32, tag="bank", name="acc")
-                nc.tensor.matmul_mx(
-                    out=acc[:],
-                    lhsT=pe_codes[:, tile_rows].bitcast(FP8X4),
-                    lhsT_scale=pe_scales[:, tile_rows],
-                    rhs=w_codes[:, cols].bitcast(FP8X4),
-                    rhs_scale=w_scales[:, cols],
-                    start=True,
-                    stop=True,
-                )
+                multiply(acc, i, blk, True, True)
                 nc.vector.scalar_tensor_tensor(
-                    out=y[:, cols], in0=acc[:], scalar=1.0, in1=b_all[:, cols],
-                    op0=ALU.mult, op1=ALU.add, accum_out=y_sums[:, blk : blk + 1],
+                    out=y[:, cols], in0=acc[:], scalar=neg_mean[:, 0:1], in1=b_all[:, cols],
+                    op0=ALU.add, op1=ALU.add,
                 )
-            y_sum = stats.tile([P, 1], F32, name="y_sum")
-            nc.vector.tensor_reduce(out=y_sum[:], in_=y_sums[:], axis=AXIS.X, op=ALU.add)
-            neg_mean = stats.tile([P, 1], F32, name="neg_mean")
-            nc.vector.tensor_scalar_mul(out=neg_mean[:], in0=y_sum[:], scalar1=-1.0 / N_OUT)
-            return y, neg_mean
+            return y
 
-        def finish(i, result, rstd):
-            for g, cols in enumerate(groups):
-                if g >= GPSIMD_GROUPS or i == ROW_TILES - 1:
-                    nc.vector.scalar_tensor_tensor(
-                        out=result[:, cols], in0=result[:, cols], scalar=rstd[:, 0:1],
-                        in1=beta_all[:, cols], op0=ALU.mult, op1=ALU.add,
-                    )
-                else:
-                    nc.scalar.mul(out=result[:, cols], in_=result[:, cols], mul=rstd[:, 0:1])
-                    nc.gpsimd.tensor_add(
-                        out=result[:, cols], in0=result[:, cols], in1=beta_all[:, cols]
-                    )
-                nc.sync.dma_start(out=out_tiles[:, i, cols], in_=result[:, cols])
-
-        y, neg_mean = product(0)
-        for cols in pieces[1:]:
-            quantise(cols)
-        earlier = None
-        for i in range(ROW_TILES + 1):
-            if i < ROW_TILES:
-                squares = scratch.tile([P, N_OUT], BF16)
-                sum_sq = stats.tile([P, 1], F32)
+        def inverse_std(y):
+            half_cols = N_OUT // 2
+            sums = []
+            for h in range(2):
+                squares = scratch.tile([P, half_cols], BF16, name="squares")
+                sum_sq = stats.tile([P, 1], F32, name="sum_sq%d" % h)
                 nc.scalar.activation(
-                    out=squares[:], in_=y[:], func=ACT.Square, bias=neg_mean[:, 0:1],
-                    accum_out=sum_sq[:],
+                    out=squares[:], in_=y[:, h * half_cols : (h + 1) * half_cols],
+                    func=ACT.Square, accum_out=sum_sq[:],
                 )
-                result = results.tile([P, N_OUT], F32)
-                for g, cols in enumerate(groups):
-                    nc.vector.scalar_tensor_tensor(
-                        out=result[:, cols], in0=y[:, cols], scalar=neg_mean[:, 0:1],
-                        in1=gamma_banks[g][:], op0=ALU.add, op1=ALU.mult,
-                    )
-            if earlier is not None:
-                rstd = stats.tile([P, 1], F32)
-                nc.vector.reciprocal(out=rstd[:], in_=earlier[1][:])
-            if i + 1 < ROW_TILES:
-                y, neg_mean = product(i + 1)
-            if earlier is not None:
-                finish(i - 1, earlier[0], rstd)
-            if i < ROW_TILES:
-                var_eps = stats.tile([P, 1], F32)
-                nc.vector.tensor_scalar(
-                    out=var_eps[:], in0=sum_sq[:], scalar1=1.0 / N_OUT, scalar2=LN_EPS,
-                    op0=ALU.mult, op1=ALU.add,
+                sums.append(sum_sq)
+            part = stats.tile([P, 1], F32, name="part")
+            nc.scalar.activation(
+                out=part[:], in_=sums[0][:], func=ACT.Identity, scale=1.0 / N_OUT, bias=eps[:, 0:1]
+            )
+            rstd = stats.tile([P, 1], F32, name="rstd")
+            nc.scalar.activation(
+                out=rstd[:], in_=sums[1][:], func=ACT.Abs_reciprocal_sqrt, scale=1.0 / N_OUT,
+                bias=part[:, 0:1],
+            )
+            return rstd
+
+        def finish(i, y, rstd):
+            for g, cols in enumerate(groups):
+                nc.vector.scalar_tensor_tensor(
+                    out=y[:, cols], in0=y[:, cols], scalar=rstd[:, 0:1],
+                    in1=gamma_banks[g][:], op0=ALU.mult, op1=ALU.mult,
                 )
-                std = stats.tile([P, 1], F32)
-                nc.scalar.activation(out=std[:], in_=var_eps[:], func=ACT.Sqrt)
-                earlier = (result, std)
+                nc.gpsimd.tensor_add(out=y[:, cols], in0=y[:, cols], in1=beta_all[:, cols])
+                nc.sync.dma_start(out=out_tiles[:, i, cols], in_=y[:, cols])
+
+        def start_row_tile(i):
+            neg_mean = stats.tile([P, 1], F32, name="neg_mean")
+            minus_mean(i, neg_mean[:], neg_b_share[:, 0:1])
+            return neg_mean
+
+        straight = [i for i in range(ROW_TILES) if i not in FLIPPED_TILES]
+        neg_mean = start_row_tile(straight[0])
+        encode(FLIPPED_ROWS)
+        quantise(FLIPPED_ROWS)
+        y = centred(straight[0], neg_mean)
+        for cols in PIECES[2:]:
+            encode(cols)
+            quantise(cols)
+        spread_gamma()
+        nc.scalar.activation(out=warm[:], in_=half_pi[:], func=ACT.Abs_reciprocal_sqrt)
+        neg_mean = start_row_tile(straight[1])
+        flipped_products(range(4))
+        for step, i in enumerate(straight):
+            rstd = inverse_std(y)
+            current = y
+            if step + 1 < len(straight):
+                y = centred(straight[step + 1], neg_mean)
+            if step + 2 < len(straight):
+                neg_mean = start_row_tile(straight[step + 2])
+            if step < 4:
+                flipped_products(range(4 + 3 * step, 4 + 3 * (step + 1)))
+            finish(i, current, rstd)
+            if step == 2:
+                for q, flipped in enumerate(FLIPPED_TILES):
+                    minus_mean(flipped, neg_p_mean[:, q : q + 1], 0.0)
+            if step == 3:
+                split_t = flipped_stats()
+            if step == 4:
+                flipped_finish(split_t, (0,))
+        flipped_finish(split_t, (1,))

@@ -11,7 +11,9 @@ U8 = mybir.dt.uint8
 FP8X4 = mybir.dt.float8_e4m3fn_x4
 ALU = mybir.AluOpType
 ACT = mybir.ActivationFunctionType
-AXIS = mybir.AxisListType
+ACTIVATION = mybir.EngineType.Activation
+DVE = mybir.EngineType.DVE
+POOL = mybir.EngineType.Pool
 
 P = 128
 PACK = 4
@@ -24,11 +26,12 @@ ROW_TILES = ROWS // P
 BANKS = N_OUT // BANK
 GAIN_BANK = 1024
 GROUPS = N_OUT // GAIN_BANK
-PIECES = (slice(0, 128), slice(128, 384), slice(384, 640), slice(640, 896), slice(896, 1024))
+PIECES = (slice(0, 128), slice(128, 256), slice(256, 512), slice(512, 768), slice(768, 1024))
 FLIPPED_ROWS = PIECES[1]
-FLIPPED_TILES = (1, 2)
+FLIPPED_TILES = (1,)
 FLIPPED_WIDTH = len(FLIPPED_TILES) * P
 OUT_BLOCKS = N_OUT // P
+UNIT = BANK // FLIPPED_WIDTH
 PARTS = 3
 MAX_COORD = 10.0
 LN_EPS = 1e-5
@@ -40,22 +43,23 @@ def tile_positionencoder_kernel(tc, state, W_words, W_scales, b, gamma, beta, ou
     nc = tc.nc
     with (
         tc.tile_pool(name="const", bufs=1) as const,
-        tc.tile_pool(name="rows", bufs=4) as rows,
+        tc.tile_pool(name="rows", bufs=5) as rows,
         tc.tile_pool(name="scratch", bufs=2) as scratch,
         tc.tile_pool(name="stats", bufs=4) as stats,
         tc.psum_pool(name="gain", bufs=1) as gain,
-        tc.psum_pool(name="psum", bufs=2) as psum,
-        tc.psum_pool(name="side", bufs=2) as side,
+        tc.psum_pool(name="psum", bufs=3) as psum,
+        tc.psum_pool(name="side", bufs=1) as side,
     ):
         state_sb = const.tile([P, ROW_TILES * COORDS], BF16)
         nc.sync.dma_start(out=state_sb[:], in_=state.rearrange("(m i) c -> m (i c)", i=ROW_TILES))
 
         by_block = const.tile([P, P], BF16)
         nc.vector.memset(by_block[:].bitcast(I32), 0)
-        nc.sync.dma_start(out=by_block[0:OUT_BLOCKS, :], in_=b.rearrange("(j p) -> j p", p=P))
-        nc.sync.dma_start(
-            out=by_block[OUT_BLOCKS : 2 * OUT_BLOCKS, :], in_=gamma.rearrange("(j p) -> j p", p=P)
-        )
+        for slot, vector in enumerate((b, gamma, beta)):
+            nc.sync.dma_start(
+                out=by_block[slot * OUT_BLOCKS : (slot + 1) * OUT_BLOCKS, :],
+                in_=vector.rearrange("(j p) -> j p", p=P),
+            )
 
         w_scales = const.tile([P, N_OUT], U8, align_bytes=64)
         nc.vector.memset(w_scales[:].bitcast(I32), 0)
@@ -155,46 +159,57 @@ def tile_positionencoder_kernel(tc, state, W_words, W_scales, b, gamma, beta, ou
                 in_=pe_grouped[:, cols, :].rearrange("p r t -> p (r t)"),
             )
 
-        encode(PIECES[0])
-        quantise(PIECES[0])
-
-        cols_t = side.tile([P, P], BF16, tag="side", name="cols_t")
-        nc.tensor.transpose(cols_t[:], by_block[:], identity_bf16[:])
-        b_bf16 = const.tile([P, OUT_BLOCKS], BF16)
-        nc.vector.tensor_copy(out=b_bf16[:], in_=cols_t[:, :OUT_BLOCKS])
+        vectors_bf16 = const.tile([P, 3, OUT_BLOCKS], BF16)
         b_cols = const.tile([P, OUT_BLOCKS], F32)
-        nc.vector.tensor_copy(out=b_cols[:], in_=cols_t[:, :OUT_BLOCKS])
-        gamma_bf16 = const.tile([P, OUT_BLOCKS], BF16)
-        nc.vector.tensor_copy(out=gamma_bf16[:], in_=cols_t[:, OUT_BLOCKS : 2 * OUT_BLOCKS])
         gamma_cols = const.tile([P, OUT_BLOCKS], F32)
-        nc.vector.tensor_copy(out=gamma_cols[:], in_=cols_t[:, OUT_BLOCKS : 2 * OUT_BLOCKS])
         b_gamma_cols = const.tile([P, OUT_BLOCKS], F32)
-        nc.vector.tensor_mul(out=b_gamma_cols[:], in0=b_cols[:], in1=gamma_cols[:])
-        b_sums = side.tile([P, OUT_BLOCKS], F32, tag="side", name="b_sums")
-        nc.tensor.matmul(out=b_sums[:], lhsT=ones[:], rhs=b_bf16[:], start=True, stop=True)
-        neg_b_share = const.tile([P, 1], F32)
-        b_ignored = const.tile([P, OUT_BLOCKS], F32)
-        nc.scalar.activation(
-            out=b_ignored[:], in_=b_sums[:], func=ACT.Copy, scale=-1.0 / (N_OUT * BANK),
-            accum_out=neg_b_share[:],
-        )
-        neg_b_mean = const.tile([P, 1], F32)
-        nc.vector.tensor_scalar_mul(out=neg_b_mean[:], in0=neg_b_share[:], scalar1=float(BANK))
         b_centred_cols = const.tile([P, OUT_BLOCKS], F32)
-        nc.vector.tensor_scalar_add(
-            out=b_centred_cols[:], in0=b_cols[:], scalar1=neg_b_mean[:, 0:1]
-        )
+        neg_b_share = const.tile([P, 1], F32)
+        neg_b_mean = const.tile([P, 1], F32)
 
-        gamma_banks = [
-            gain.tile([P, GAIN_BANK], BF16, name="gamma_bank%d" % g) for g in range(GROUPS)
-        ]
+        def turn_vectors():
+            cols_t = side.tile([P, P], BF16, tag="side", name="cols_t")
+            nc.tensor.transpose(cols_t[:], by_block[:], identity_bf16[:])
+            nc.vector.tensor_copy(
+                out=vectors_bf16[:].rearrange("p v j -> p (v j)"), in_=cols_t[:, : 3 * OUT_BLOCKS]
+            )
+            nc.vector.tensor_copy(out=b_cols[:], in_=cols_t[:, :OUT_BLOCKS])
+            nc.vector.tensor_copy(out=gamma_cols[:], in_=cols_t[:, OUT_BLOCKS : 2 * OUT_BLOCKS])
+
+        def mean_of_b():
+            b_sums = side.tile([P, OUT_BLOCKS], F32, tag="side", name="b_sums")
+            nc.tensor.matmul(out=b_sums[:], lhsT=ones[:], rhs=vectors_bf16[:, 0, :], start=True, stop=True)
+            b_ignored = const.tile([P, OUT_BLOCKS], F32)
+            nc.scalar.activation(
+                out=b_ignored[:], in_=b_sums[:], func=ACT.Copy, scale=-1.0 / (N_OUT * BANK),
+                accum_out=neg_b_share[:],
+            )
+
+        def flipped_constants():
+            nc.vector.tensor_mul(out=b_gamma_cols[:], in0=b_cols[:], in1=gamma_cols[:])
+            nc.vector.tensor_scalar_mul(
+                out=neg_b_mean[:], in0=neg_b_share[:], scalar1=float(BANK)
+            )
+            nc.vector.tensor_scalar_add(
+                out=b_centred_cols[:], in0=b_cols[:], scalar1=neg_b_mean[:, 0:1]
+            )
+
+        gamma_tags = ["gamma_bank%d" % g for g in range(GROUPS)]
 
         def spread_gamma():
-            for j in range(OUT_BLOCKS):
-                g, h = divmod(j, GAIN_BANK // P)
+            banks = []
+            for g in range(GROUPS):
+                gamma_bank = gain.tile([P, GAIN_BANK], BF16, tag=gamma_tags[g], name="gamma_bank")
+                spread(gamma_bank, 1, g)
+                banks.append(gamma_bank)
+            return banks
+
+        def spread(bank, vector, g):
+            for h in range(GAIN_BANK // P):
+                j = g * (GAIN_BANK // P) + h
                 nc.tensor.transpose(
-                    gamma_banks[g][:, h * P : (h + 1) * P],
-                    gamma_bf16[:, j : j + 1].to_broadcast([P, P]),
+                    bank[:, h * P : (h + 1) * P],
+                    vectors_bf16[:, vector, j : j + 1].to_broadcast([P, P]),
                     identity_bf16[:],
                 )
 
@@ -214,122 +229,146 @@ def tile_positionencoder_kernel(tc, state, W_words, W_scales, b, gamma, beta, ou
                 stop=stop,
             )
 
-        def minus_mean(i, neg_mean, share):
-            total = side.tile([P, BANK], F32, tag="side", name="total")
+        def total_of(i, early_bank=None):
+            if early_bank is None:
+                total = psum.tile([P, BANK], F32, tag="bank", name="total")
+            else:
+                total = gain.tile([P, BANK], F32, tag=early_bank, name="early_total")
             for blk in range(BANKS):
                 multiply(total, i, blk, blk == 0, blk == BANKS - 1)
+            return total
+
+        def minus_mean(total, neg_mean, share):
             ignored = scratch.tile([P, BANK], BF16, name="ignored")
             nc.scalar.activation(
                 out=ignored[:], in_=total[:], func=ACT.Identity, scale=-1.0 / N_OUT,
                 bias=share, accum_out=neg_mean,
             )
 
+        def minus_mean_of_y(total):
+            neg_mean = stats.tile([P, 1], F32, name="neg_mean")
+            minus_mean(total, neg_mean[:], neg_b_share[:, 0:1])
+            return neg_mean
+
         scaled = const.tile([P, OUT_BLOCKS, FLIPPED_WIDTH], F32)
         squared = const.tile([P, OUT_BLOCKS, FLIPPED_WIDTH], F32)
 
-        def flipped_products(pairs):
-            for pair in pairs:
-                acc = side.tile([P, 2, FLIPPED_WIDTH], F32, tag="side", name="flipped_acc")
-                for h in range(2):
-                    j = 2 * pair + h
-                    cols = slice(j * P, (j + 1) * P)
-                    nc.tensor.matmul_mx(
-                        out=acc[:, h, :],
-                        lhsT=w_codes[:, cols].bitcast(FP8X4),
-                        lhsT_scale=w_scales[:, cols],
-                        rhs=pe_codes[:, FLIPPED_ROWS].bitcast(FP8X4),
-                        rhs_scale=pe_scales[:, FLIPPED_ROWS],
-                        start=True,
-                        stop=True,
-                    )
-                for h in range(2):
-                    j = 2 * pair + h
-                    nc.scalar.activation(
-                        out=squared[:, j, :], in_=acc[:, h, :], func=ACT.Square,
-                        bias=b_centred_cols[:, j : j + 1],
-                    )
-                    nc.scalar.activation(
-                        out=scaled[:, j, :], in_=acc[:, h, :], func=ACT.Identity,
-                        scale=gamma_cols[:, j : j + 1], bias=b_gamma_cols[:, j : j + 1],
-                    )
+        def flipped_products(unit):
+            acc = side.tile([P, UNIT, FLIPPED_WIDTH], F32, tag="side", name="flipped_acc")
+            for h in range(UNIT):
+                j = UNIT * unit + h
+                cols = slice(j * P, (j + 1) * P)
+                nc.tensor.matmul_mx(
+                    out=acc[:, h, :],
+                    lhsT=w_codes[:, cols].bitcast(FP8X4),
+                    lhsT_scale=w_scales[:, cols],
+                    rhs=pe_codes[:, FLIPPED_ROWS].bitcast(FP8X4),
+                    rhs_scale=pe_scales[:, FLIPPED_ROWS],
+                    start=True,
+                    stop=True,
+                )
+            for h in range(UNIT):
+                j = UNIT * unit + h
+                nc.scalar.activation(
+                    out=squared[:, j, :], in_=acc[:, h, :], func=ACT.Square,
+                    bias=b_centred_cols[:, j : j + 1],
+                )
+                nc.scalar.activation(
+                    out=scaled[:, j, :], in_=acc[:, h, :], func=ACT.Identity,
+                    scale=gamma_cols[:, j : j + 1], bias=b_gamma_cols[:, j : j + 1],
+                )
 
         neg_p_mean = const.tile([P, len(FLIPPED_TILES)], F32)
         flipped_rstd = const.tile([P, len(FLIPPED_TILES)], F32)
 
-        def flipped_stats():
-            mean_sq = const.tile([P, len(FLIPPED_TILES)], F32)
-            for q in range(len(FLIPPED_TILES)):
-                sums = side.tile([P, P], F32, tag="side", name="sums")
-                for j in range(OUT_BLOCKS):
-                    nc.tensor.matmul(
-                        out=sums[:], lhsT=squared[:, j, q * P : (q + 1) * P], rhs=identity[:],
-                        is_transpose=True, start=(j == 0), stop=(j == OUT_BLOCKS - 1),
-                    )
-                ignored = scratch.tile([P, BANK], BF16, name="ignored")
-                nc.scalar.activation(
-                    out=ignored[:, :P], in_=sums[:], func=ACT.Copy, scale=1.0 / N_OUT,
-                    accum_out=mean_sq[:, q : q + 1],
+        mean_sq = const.tile([P, len(FLIPPED_TILES)], F32)
+        mean_p_sq = const.tile([P, len(FLIPPED_TILES)], F32)
+        var_eps = const.tile([P, len(FLIPPED_TILES)], F32)
+        rest = const.tile([P, len(FLIPPED_TILES), 2], F32)
+        split_t = const.tile([P, len(FLIPPED_TILES), P], BF16)
+
+        def flipped_sums(q):
+            sums = side.tile([P, P], F32, tag="side", name="sums")
+            for j in range(OUT_BLOCKS):
+                nc.tensor.matmul(
+                    out=sums[:], lhsT=squared[:, j, q * P : (q + 1) * P], rhs=identity[:],
+                    is_transpose=True, start=(j == 0), stop=(j == OUT_BLOCKS - 1),
                 )
-            mean_p_sq = const.tile([P, len(FLIPPED_TILES)], F32)
-            nc.vector.tensor_mul(out=mean_p_sq[:], in0=neg_p_mean[:], in1=neg_p_mean[:])
-            var_eps = const.tile([P, len(FLIPPED_TILES)], F32)
-            nc.vector.scalar_tensor_tensor(
-                out=var_eps[:], in0=mean_sq[:], scalar=LN_EPS, in1=mean_p_sq[:],
-                op0=ALU.add, op1=ALU.subtract,
+            ignored = scratch.tile([P, BANK], BF16, name="ignored")
+            nc.scalar.activation(
+                out=ignored[:, :P], in_=sums[:], func=ACT.Copy, scale=1.0 / N_OUT,
+                accum_out=mean_sq[:, q : q + 1],
             )
+
+        def flipped_rstds():
+            nc.gpsimd.tensor_mul(out=mean_p_sq[:], in0=neg_p_mean[:], in1=neg_p_mean[:])
+            nc.gpsimd.tensor_scalar_add(out=var_eps[:], in0=mean_sq[:], scalar1=LN_EPS)
+            nc.gpsimd.tensor_sub(out=var_eps[:], in0=var_eps[:], in1=mean_p_sq[:])
             nc.scalar.activation(
                 out=flipped_rstd[:], in_=var_eps[:], func=ACT.Abs_reciprocal_sqrt
             )
-            rest = const.tile([P, len(FLIPPED_TILES), 2], F32)
-            nc.vector.tensor_scalar_add(
+
+        def flipped_split():
+            nc.gpsimd.tensor_scalar_add(
                 out=rest[:, :, 0], in0=neg_p_mean[:], scalar1=neg_b_mean[:, 0:1]
             )
-            nc.vector.tensor_mul(out=rest[:, :, 1], in0=var_eps[:], in1=flipped_rstd[:])
+            nc.gpsimd.tensor_mul(out=rest[:, :, 1], in0=var_eps[:], in1=flipped_rstd[:])
             parts = split[:, :, : 2 * PARTS].rearrange("m q (v s) -> m q v s", s=PARTS)
             for s in range(PARTS):
-                nc.vector.tensor_copy(out=parts[:, :, :, s], in_=rest[:])
+                nc.gpsimd.tensor_copy(out=parts[:, :, :, s], in_=rest[:])
                 if s + 1 < PARTS:
-                    nc.vector.tensor_sub(out=rest[:], in0=rest[:], in1=parts[:, :, :, s])
-            split_t = const.tile([P, len(FLIPPED_TILES), P], BF16)
+                    nc.gpsimd.tensor_sub(out=rest[:], in0=rest[:], in1=parts[:, :, :, s])
+
+        def flipped_turn():
             for q in range(len(FLIPPED_TILES)):
                 turned = side.tile([P, P], BF16, tag="side", name="turned")
                 nc.tensor.transpose(turned[:], split[:, q, :], identity_bf16[:])
                 nc.scalar.copy(out=split_t[:, q, :], in_=turned[:])
-            return split_t
 
-        def flipped_finish(split_t, tiles):
-            for q in tiles:
-                i = FLIPPED_TILES[q]
-                result = rows.tile([P, N_OUT], F32, tag="y", name="result")
-                for blk in range(BANKS):
-                    cols = slice(blk * BANK, (blk + 1) * BANK)
-                    acc = side.tile([P, BANK], F32, tag="side", name="turned_acc")
-                    nc.tensor.matmul(
-                        out=acc[:], lhsT=split_t[:, q, :], rhs=vectors[:, cols],
-                        start=True, stop=False,
-                    )
-                    for h in range(BANK // P):
-                        nc.tensor.matmul(
-                            out=acc[:, h * P : (h + 1) * P],
-                            lhsT=scaled[:, blk * (BANK // P) + h, q * P : (q + 1) * P],
-                            rhs=identity[:], is_transpose=True, start=False,
-                            stop=(h == BANK // P - 1),
-                        )
-                    if blk % 2 == 0 or q == 0:
-                        nc.scalar.mul(
-                            out=result[:, cols], in_=acc[:], mul=flipped_rstd[:, q : q + 1]
-                        )
-                    else:
-                        nc.vector.tensor_scalar_mul(
-                            out=result[:, cols], in0=acc[:], scalar1=flipped_rstd[:, q : q + 1]
-                        )
-                    if blk % 2 == 1:
-                        stored = slice((blk - 1) * BANK, (blk + 1) * BANK)
-                        nc.sync.dma_start(out=out_tiles[:, i, stored], in_=result[:, stored])
+        results = {}
 
-        def centred(i, neg_mean):
-            y = rows.tile([P, N_OUT], F32, tag="y", name="y")
-            for blk in range(BANKS):
+        def flipped_finish(q, blk, on_vector):
+            if blk == 0:
+                results[q] = rows.tile([P, N_OUT], F32, tag="y", name="result")
+            result = results[q]
+            cols = slice(blk * BANK, (blk + 1) * BANK)
+            acc = side.tile([P, BANK], F32, tag="side", name="turned_acc")
+            nc.tensor.matmul(
+                out=acc[:], lhsT=split_t[:, q, :], rhs=vectors[:, cols], start=True, stop=False
+            )
+            for h in range(BANK // P):
+                nc.tensor.matmul(
+                    out=acc[:, h * P : (h + 1) * P],
+                    lhsT=scaled[:, blk * (BANK // P) + h, q * P : (q + 1) * P],
+                    rhs=identity[:], is_transpose=True, start=False, stop=(h == BANK // P - 1),
+                )
+            rstd = flipped_rstd[:, q : q + 1]
+            if on_vector:
+                nc.vector.tensor_scalar_mul(out=result[:, cols], in0=acc[:], scalar1=rstd)
+            else:
+                nc.scalar.mul(out=result[:, cols], in_=acc[:], mul=rstd)
+            if blk % 2 == 1:
+                stored = slice((blk - 1) * BANK, (blk + 1) * BANK)
+                nc.sync.dma_start(out=out_tiles[:, FLIPPED_TILES[q], stored], in_=result[:, stored])
+
+        def inverse_std(y, half, earlier):
+            half_cols = N_OUT // 2
+            squares = scratch.tile([P, half_cols], BF16, name="squares")
+            sum_sq = stats.tile([P, 1], F32, name="sum_sq%d" % half)
+            nc.scalar.activation(
+                out=squares[:], in_=y[:, half * half_cols : (half + 1) * half_cols],
+                func=ACT.Square, accum_out=sum_sq[:],
+            )
+            answer = stats.tile([P, 1], F32, name="answer%d" % half)
+            nc.scalar.activation(
+                out=answer[:], in_=sum_sq[:], scale=1.0 / N_OUT,
+                func=ACT.Abs_reciprocal_sqrt if half else ACT.Identity,
+                bias=earlier[:, 0:1],
+            )
+            return answer
+
+        def centred(i, y, neg_mean, banks):
+            for blk in banks:
                 cols = slice(blk * BANK, (blk + 1) * BANK)
                 acc = psum.tile([P, BANK], F32, tag="bank", name="acc")
                 multiply(acc, i, blk, True, True)
@@ -337,71 +376,73 @@ def tile_positionencoder_kernel(tc, state, W_words, W_scales, b, gamma, beta, ou
                     out=y[:, cols], in0=acc[:], scalar=neg_mean[:, 0:1], in1=b_all[:, cols],
                     op0=ALU.add, op1=ALU.add,
                 )
+
+        def new_row_tile():
+            y = rows.tile([P, N_OUT], F32, tag="y", name="y")
             return y
 
-        def inverse_std(y):
-            half_cols = N_OUT // 2
-            sums = []
-            for h in range(2):
-                squares = scratch.tile([P, half_cols], BF16, name="squares")
-                sum_sq = stats.tile([P, 1], F32, name="sum_sq%d" % h)
-                nc.scalar.activation(
-                    out=squares[:], in_=y[:, h * half_cols : (h + 1) * half_cols],
-                    func=ACT.Square, accum_out=sum_sq[:],
-                )
-                sums.append(sum_sq)
-            part = stats.tile([P, 1], F32, name="part")
-            nc.scalar.activation(
-                out=part[:], in_=sums[0][:], func=ACT.Identity, scale=1.0 / N_OUT, bias=eps[:, 0:1]
-            )
-            rstd = stats.tile([P, 1], F32, name="rstd")
-            nc.scalar.activation(
-                out=rstd[:], in_=sums[1][:], func=ACT.Abs_reciprocal_sqrt, scale=1.0 / N_OUT,
-                bias=part[:, 0:1],
-            )
-            return rstd
-
-        def finish(i, y, rstd):
+        def finish(i, y, rstd, last, after_first):
             for g, cols in enumerate(groups):
                 nc.vector.scalar_tensor_tensor(
                     out=y[:, cols], in0=y[:, cols], scalar=rstd[:, 0:1],
                     in1=gamma_banks[g][:], op0=ALU.mult, op1=ALU.mult,
                 )
-                nc.gpsimd.tensor_add(out=y[:, cols], in0=y[:, cols], in1=beta_all[:, cols])
+                if last and g > 0:
+                    beta_bank = psum.tile([P, GAIN_BANK], BF16, tag="bank", name="beta_bank")
+                    spread(beta_bank, 2, g)
+                    nc.vector.tensor_add(out=y[:, cols], in0=y[:, cols], in1=beta_bank[:])
+                else:
+                    nc.gpsimd.tensor_add(out=y[:, cols], in0=y[:, cols], in1=beta_all[:, cols])
                 nc.sync.dma_start(out=out_tiles[:, i, cols], in_=y[:, cols])
-
-        def start_row_tile(i):
-            neg_mean = stats.tile([P, 1], F32, name="neg_mean")
-            minus_mean(i, neg_mean[:], neg_b_share[:, 0:1])
-            return neg_mean
+                if g == 0:
+                    for call in after_first:
+                        call()
 
         straight = [i for i in range(ROW_TILES) if i not in FLIPPED_TILES]
-        neg_mean = start_row_tile(straight[0])
-        encode(FLIPPED_ROWS)
-        quantise(FLIPPED_ROWS)
-        y = centred(straight[0], neg_mean)
-        for cols in PIECES[2:]:
-            encode(cols)
-            quantise(cols)
-        spread_gamma()
-        nc.scalar.activation(out=warm[:], in_=half_pi[:], func=ACT.Abs_reciprocal_sqrt)
-        neg_mean = start_row_tile(straight[1])
-        flipped_products(range(4))
-        for step, i in enumerate(straight):
-            rstd = inverse_std(y)
-            current = y
-            if step + 1 < len(straight):
-                y = centred(straight[step + 1], neg_mean)
-            if step + 2 < len(straight):
-                neg_mean = start_row_tile(straight[step + 2])
-            if step < 4:
-                flipped_products(range(4 + 3 * step, 4 + 3 * (step + 1)))
-            finish(i, current, rstd)
-            if step == 2:
-                for q, flipped in enumerate(FLIPPED_TILES):
-                    minus_mean(flipped, neg_p_mean[:, q : q + 1], 0.0)
-            if step == 3:
-                split_t = flipped_stats()
-            if step == 4:
-                flipped_finish(split_t, (0,))
-        flipped_finish(split_t, (1,))
+        units = list(range(OUT_BLOCKS // UNIT))
+
+        def take_units(count):
+            for unit in units[:count]:
+                flipped_products(unit)
+            for unit in units[:count]:
+                units.remove(unit)
+
+        with tc.manual_schedule(engines={ACTIVATION, DVE, POOL}):
+            encode(FLIPPED_ROWS)
+            turn_vectors()
+            mean_of_b()
+            quantise(FLIPPED_ROWS)
+            encode(PIECES[0])
+            quantise(PIECES[0])
+            flipped_constants()
+            for cols in PIECES[2:]:
+                encode(cols)
+                quantise(cols)
+            take_units(2)
+            neg_mean = minus_mean_of_y(total_of(straight[0], gamma_tags[2]))
+            nc.scalar.activation(out=warm[:], in_=half_pi[:], func=ACT.Abs_reciprocal_sqrt)
+            y = new_row_tile()
+            centred(straight[0], y, neg_mean, range(BANKS))
+            neg_mean = minus_mean_of_y(total_of(straight[1], gamma_tags[3]))
+            gamma_banks = spread_gamma()
+            rstd = inverse_std(y, 1, inverse_std(y, 0, eps))
+            for step, i in enumerate(straight):
+                current, current_rstd = y, rstd
+                ahead = straight[step + 1 :]
+                after_first = []
+                if ahead:
+                    y = new_row_tile()
+                    centred(ahead[0], y, neg_mean, range(BANKS))
+                    rstd = inverse_std(y, 1, inverse_std(y, 0, eps))
+                if len(ahead) > 1:
+                    neg_mean = minus_mean_of_y(total_of(ahead[1]))
+                take_units(2)
+                if step == 2:
+                    minus_mean(total_of(FLIPPED_TILES[0]), neg_p_mean[:], 0.0)
+                if step == 3:
+                    flipped_sums(0)
+                    after_first = [flipped_rstds, flipped_split, flipped_turn]
+                finish(i, current, current_rstd, not ahead, after_first)
+                if step in (4, 5):
+                    for blk in range(BANKS // 2):
+                        flipped_finish(0, blk + (step - 4) * BANKS // 2, False)

@@ -133,9 +133,9 @@ def tile_positionencoder_kernel(tc, state, W_words, W_scales, b, gamma, beta, ou
         pe_codes = const.tile([P, ROWS], U32, align_bytes=64)
         pe_scales = const.tile([P, ROWS], U8, align_bytes=64)
 
-        def encode(cols):
+        def turn_state(cols, pool, tag):
             count = cols.stop - cols.start
-            s_t = psum.tile([P, count], F32, tag="bank", name="s_t")
+            s_t = pool.tile([P, count], F32, tag=tag, name="s_t")
             for q in range(count // P):
                 i = cols.start // P + q
                 nc.tensor.transpose(
@@ -143,6 +143,9 @@ def tile_positionencoder_kernel(tc, state, W_words, W_scales, b, gamma, beta, ou
                     s_wide[:, i * COORDS : (i + 1) * COORDS, :].rearrange("m c e -> m (c e)"),
                     identity[:],
                 )
+            return s_t
+
+        def encode(cols, s_t):
             for t in range(PACK):
                 nc.scalar.activation(
                     out=pe_planes[:, t, cols], in_=s_t[:], func=ACT.Sin,
@@ -254,7 +257,8 @@ def tile_positionencoder_kernel(tc, state, W_words, W_scales, b, gamma, beta, ou
         squared = const.tile([P, OUT_BLOCKS, FLIPPED_WIDTH], F32)
 
         def flipped_products(unit):
-            acc = side.tile([P, UNIT, FLIPPED_WIDTH], F32, tag="side", name="flipped_acc")
+            pool, tag = (gain, gamma_tags[0]) if unit == 1 else (side, "side")
+            acc = pool.tile([P, UNIT, FLIPPED_WIDTH], F32, tag=tag, name="flipped_acc")
             for h in range(UNIT):
                 j = UNIT * unit + h
                 cols = slice(j * P, (j + 1) * P)
@@ -282,9 +286,7 @@ def tile_positionencoder_kernel(tc, state, W_words, W_scales, b, gamma, beta, ou
         flipped_rstd = const.tile([P, len(FLIPPED_TILES)], F32)
 
         mean_sq = const.tile([P, len(FLIPPED_TILES)], F32)
-        mean_p_sq = const.tile([P, len(FLIPPED_TILES)], F32)
-        var_eps = const.tile([P, len(FLIPPED_TILES)], F32)
-        rest = const.tile([P, len(FLIPPED_TILES), 2], F32)
+        rest = const.tile([P, PARTS + 3, 2], F32)
         split_t = const.tile([P, len(FLIPPED_TILES), P], BF16)
 
         def flipped_sums(q):
@@ -300,24 +302,41 @@ def tile_positionencoder_kernel(tc, state, W_words, W_scales, b, gamma, beta, ou
                 accum_out=mean_sq[:, q : q + 1],
             )
 
-        def flipped_rstds():
-            nc.gpsimd.tensor_mul(out=mean_p_sq[:], in0=neg_p_mean[:], in1=neg_p_mean[:])
-            nc.gpsimd.tensor_scalar_add(out=var_eps[:], in0=mean_sq[:], scalar1=LN_EPS)
-            nc.gpsimd.tensor_sub(out=var_eps[:], in0=var_eps[:], in1=mean_p_sq[:])
+        def split_value(q, v):
+            for s in range(PARTS):
+                part = split[:, q, v * PARTS + s : v * PARTS + s + 1]
+                left = rest[:, s, v : v + 1]
+                nc.scalar.copy(out=part, in_=left)
+                if s + 1 < PARTS:
+                    nc.scalar.activation(
+                        out=rest[:, s + 1, v : v + 1], in_=part, func=ACT.Identity, scale=-1.0,
+                        bias=left,
+                    )
+
+        def flipped_mean(q):
+            mean = neg_p_mean[:, q : q + 1]
             nc.scalar.activation(
-                out=flipped_rstd[:], in_=var_eps[:], func=ACT.Abs_reciprocal_sqrt
+                out=rest[:, 0, 0:1], in_=mean, func=ACT.Identity, bias=neg_b_mean[:, 0:1]
+            )
+            split_value(q, 0)
+            nc.scalar.mul(out=rest[:, PARTS, 0:1], in_=mean, mul=-1.0)
+            nc.scalar.activation(
+                out=rest[:, PARTS + 1, 0:1], in_=mean, func=ACT.Identity,
+                scale=rest[:, PARTS, 0:1], bias=eps[:, 0:1],
             )
 
-        def flipped_split():
-            nc.gpsimd.tensor_scalar_add(
-                out=rest[:, :, 0], in0=neg_p_mean[:], scalar1=neg_b_mean[:, 0:1]
+        def flipped_std(q):
+            eps_less = rest[:, PARTS + 1, 0:1]
+            rstd = flipped_rstd[:, q : q + 1]
+            nc.scalar.activation(
+                out=rstd, in_=mean_sq[:, q : q + 1], func=ACT.Abs_reciprocal_sqrt, bias=eps_less
             )
-            nc.gpsimd.tensor_mul(out=rest[:, :, 1], in0=var_eps[:], in1=flipped_rstd[:])
-            parts = split[:, :, : 2 * PARTS].rearrange("m q (v s) -> m q v s", s=PARTS)
-            for s in range(PARTS):
-                nc.gpsimd.tensor_copy(out=parts[:, :, :, s], in_=rest[:])
-                if s + 1 < PARTS:
-                    nc.gpsimd.tensor_sub(out=rest[:], in0=rest[:], in1=parts[:, :, :, s])
+            nc.scalar.activation(
+                out=rest[:, PARTS + 2, 0:1], in_=mean_sq[:, q : q + 1], func=ACT.Identity,
+                bias=eps_less,
+            )
+            nc.scalar.mul(out=rest[:, 0, 1:2], in_=rest[:, PARTS + 2, 0:1], mul=rstd)
+            split_value(q, 1)
 
         def flipped_turn():
             for q in range(len(FLIPPED_TILES)):
@@ -381,7 +400,7 @@ def tile_positionencoder_kernel(tc, state, W_words, W_scales, b, gamma, beta, ou
             y = rows.tile([P, N_OUT], F32, tag="y", name="y")
             return y
 
-        def finish(i, y, rstd, last, after_first):
+        def finish(i, y, rstd, last):
             for g, cols in enumerate(groups):
                 nc.vector.scalar_tensor_tensor(
                     out=y[:, cols], in0=y[:, cols], scalar=rstd[:, 0:1],
@@ -394,9 +413,6 @@ def tile_positionencoder_kernel(tc, state, W_words, W_scales, b, gamma, beta, ou
                 else:
                     nc.gpsimd.tensor_add(out=y[:, cols], in0=y[:, cols], in1=beta_all[:, cols])
                 nc.sync.dma_start(out=out_tiles[:, i, cols], in_=y[:, cols])
-                if g == 0:
-                    for call in after_first:
-                        call()
 
         straight = [i for i in range(ROW_TILES) if i not in FLIPPED_TILES]
         units = list(range(OUT_BLOCKS // UNIT))
@@ -408,41 +424,57 @@ def tile_positionencoder_kernel(tc, state, W_words, W_scales, b, gamma, beta, ou
                 units.remove(unit)
 
         with tc.manual_schedule(engines={ACTIVATION, DVE, POOL}):
-            encode(FLIPPED_ROWS)
+            banks = [(psum, "bank")] * 3 + [(gain, gamma_tags[0]), (gain, gamma_tags[1])]
+            turned = [turn_state(cols, *bank) for cols, bank in zip(PIECES, banks)]
+            encode(PIECES[0], turned[0])
             turn_vectors()
-            mean_of_b()
-            quantise(FLIPPED_ROWS)
-            encode(PIECES[0])
             quantise(PIECES[0])
-            flipped_constants()
-            for cols in PIECES[2:]:
-                encode(cols)
+            total = total_of(straight[0], gamma_tags[2])
+            mean_of_b()
+            for cols, s_t in zip(PIECES[1:], turned[1:]):
+                encode(cols, s_t)
                 quantise(cols)
-            take_units(2)
-            neg_mean = minus_mean_of_y(total_of(straight[0], gamma_tags[2]))
+            flipped_constants()
+            neg_mean = minus_mean_of_y(total)
             nc.scalar.activation(out=warm[:], in_=half_pi[:], func=ACT.Abs_reciprocal_sqrt)
             y = new_row_tile()
             centred(straight[0], y, neg_mean, range(BANKS))
-            neg_mean = minus_mean_of_y(total_of(straight[1], gamma_tags[3]))
+            total = total_of(straight[1], gamma_tags[3])
+            take_units(2)
+            neg_mean = minus_mean_of_y(total)
             gamma_banks = spread_gamma()
             rstd = inverse_std(y, 1, inverse_std(y, 0, eps))
+            blocks = list(range(BANKS))
+
+            def finish_blocks(count):
+                for blk in blocks[:count]:
+                    flipped_finish(0, blk, False)
+                for blk in blocks[:count]:
+                    blocks.remove(blk)
+
             for step, i in enumerate(straight):
                 current, current_rstd = y, rstd
                 ahead = straight[step + 1 :]
-                after_first = []
+                take_units(1)
                 if ahead:
                     y = new_row_tile()
-                    centred(ahead[0], y, neg_mean, range(BANKS))
-                    rstd = inverse_std(y, 1, inverse_std(y, 0, eps))
+                    centred(ahead[0], y, neg_mean, range(BANKS // 2))
+                    half = inverse_std(y, 0, eps)
+                take_units(1)
+                if ahead:
+                    centred(ahead[0], y, neg_mean, range(BANKS // 2, BANKS))
+                    rstd = inverse_std(y, 1, half)
+                if step == 3:
+                    flipped_turn()
                 if len(ahead) > 1:
                     neg_mean = minus_mean_of_y(total_of(ahead[1]))
-                take_units(2)
-                if step == 2:
+                take_units(1)
+                if step == 1:
                     minus_mean(total_of(FLIPPED_TILES[0]), neg_p_mean[:], 0.0)
-                if step == 3:
+                if step == 2:
+                    flipped_mean(0)
                     flipped_sums(0)
-                    after_first = [flipped_rstds, flipped_split, flipped_turn]
-                finish(i, current, current_rstd, not ahead, after_first)
-                if step in (4, 5):
-                    for blk in range(BANKS // 2):
-                        flipped_finish(0, blk + (step - 4) * BANKS // 2, False)
+                    flipped_std(0)
+                if step >= 3:
+                    finish_blocks(2)
+                finish(i, current, current_rstd, not ahead)

@@ -435,8 +435,8 @@ def tile_positionencoder_kernel(tc, state, W_words, W_scales, b, gamma, beta, ou
                 encode(cols, s_t)
                 quantise(cols)
             flipped_constants()
-            neg_mean = minus_mean_of_y(total)
             nc.scalar.activation(out=warm[:], in_=half_pi[:], func=ACT.Abs_reciprocal_sqrt)
+            neg_mean = minus_mean_of_y(total)
             y = new_row_tile()
             centred(straight[0], y, neg_mean, range(BANKS))
             total = total_of(straight[1], gamma_tags[3])
@@ -468,7 +468,6 @@ def tile_positionencoder_kernel(tc, state, W_words, W_scales, b, gamma, beta, ou
                     flipped_turn()
                 if len(ahead) > 1:
                     neg_mean = minus_mean_of_y(total_of(ahead[1]))
-                take_units(1)
                 if step == 1:
                     minus_mean(total_of(FLIPPED_TILES[0]), neg_p_mean[:], 0.0)
                 if step == 2:

@@ -277,10 +277,12 @@ def tile_positionencoder_kernel(tc, state, W_words, W_scales, b, gamma, beta, ou
                     out=squared[:, j, :], in_=acc[:, h, :], func=ACT.Square,
                     bias=b_centred_cols[:, j : j + 1],
                 )
+                next_column()
                 nc.scalar.activation(
                     out=scaled[:, j, :], in_=acc[:, h, :], func=ACT.Identity,
                     scale=gamma_cols[:, j : j + 1], bias=b_gamma_cols[:, j : j + 1],
                 )
+                next_column()
 
         neg_p_mean = const.tile([P, len(FLIPPED_TILES)], F32)
         flipped_rstd = const.tile([P, len(FLIPPED_TILES)], F32)
@@ -302,40 +304,49 @@ def tile_positionencoder_kernel(tc, state, W_words, W_scales, b, gamma, beta, ou
                 accum_out=mean_sq[:, q : q + 1],
             )
 
+        waiting = []
+
+        def next_column():
+            for call in waiting[:1]:
+                call()
+            for call in waiting[:1]:
+                waiting.remove(call)
+
+        def all_columns():
+            for call in waiting:
+                call()
+            waiting.clear()
+
+        def put(out_col, in_col, func=ACT.Identity, scale=1.0, bias=0.0):
+            waiting.append(
+                lambda: nc.scalar.activation(
+                    out=out_col, in_=in_col, func=func, scale=scale, bias=bias
+                )
+            )
+
         def split_value(q, v):
             for s in range(PARTS):
                 part = split[:, q, v * PARTS + s : v * PARTS + s + 1]
                 left = rest[:, s, v : v + 1]
-                nc.scalar.copy(out=part, in_=left)
+                put(part, left, func=ACT.Copy)
                 if s + 1 < PARTS:
-                    nc.scalar.activation(
-                        out=rest[:, s + 1, v : v + 1], in_=part, func=ACT.Identity, scale=-1.0,
-                        bias=left,
-                    )
+                    put(rest[:, s + 1, v : v + 1], part, scale=-1.0, bias=left)
 
         def flipped_mean(q):
             mean = neg_p_mean[:, q : q + 1]
-            nc.scalar.activation(
-                out=rest[:, 0, 0:1], in_=mean, func=ACT.Identity, bias=neg_b_mean[:, 0:1]
-            )
+            p_mean = rest[:, PARTS, 0:1]
+            put(rest[:, 0, 0:1], mean, bias=neg_b_mean[:, 0:1])
+            put(p_mean, mean, func=ACT.Copy, scale=-1.0)
             split_value(q, 0)
-            nc.scalar.mul(out=rest[:, PARTS, 0:1], in_=mean, mul=-1.0)
-            nc.scalar.activation(
-                out=rest[:, PARTS + 1, 0:1], in_=mean, func=ACT.Identity,
-                scale=rest[:, PARTS, 0:1], bias=eps[:, 0:1],
-            )
+            put(rest[:, PARTS + 1, 0:1], mean, scale=p_mean, bias=eps[:, 0:1])
 
         def flipped_std(q):
             eps_less = rest[:, PARTS + 1, 0:1]
             rstd = flipped_rstd[:, q : q + 1]
-            nc.scalar.activation(
-                out=rstd, in_=mean_sq[:, q : q + 1], func=ACT.Abs_reciprocal_sqrt, bias=eps_less
-            )
-            nc.scalar.activation(
-                out=rest[:, PARTS + 2, 0:1], in_=mean_sq[:, q : q + 1], func=ACT.Identity,
-                bias=eps_less,
-            )
-            nc.scalar.mul(out=rest[:, 0, 1:2], in_=rest[:, PARTS + 2, 0:1], mul=rstd)
+            mean_square = mean_sq[:, q : q + 1]
+            put(rstd, mean_square, func=ACT.Abs_reciprocal_sqrt, bias=eps_less)
+            put(rest[:, PARTS + 2, 0:1], mean_square, bias=eps_less)
+            put(rest[:, 0, 1:2], rest[:, PARTS + 2, 0:1], scale=rstd)
             split_value(q, 1)
 
         def flipped_turn():
@@ -400,7 +411,7 @@ def tile_positionencoder_kernel(tc, state, W_words, W_scales, b, gamma, beta, ou
             y = rows.tile([P, N_OUT], F32, tag="y", name="y")
             return y
 
-        def finish(i, y, rstd, last):
+        def finish(i, y, rstd, first, last):
             for g, cols in enumerate(groups):
                 nc.vector.scalar_tensor_tensor(
                     out=y[:, cols], in0=y[:, cols], scalar=rstd[:, 0:1],
@@ -410,7 +421,12 @@ def tile_positionencoder_kernel(tc, state, W_words, W_scales, b, gamma, beta, ou
                     beta_bank = psum.tile([P, GAIN_BANK], BF16, tag="bank", name="beta_bank")
                     spread(beta_bank, 2, g)
                     nc.vector.tensor_add(out=y[:, cols], in0=y[:, cols], in1=beta_bank[:])
+                elif first or last:
+                    nc.gpsimd.tensor_add(out=y[:, cols], in0=y[:, cols], in1=beta_all[:, cols])
                 else:
+                    if g % 2 == 0:
+                        continue
+                    cols = slice((g - 1) * GAIN_BANK, (g + 1) * GAIN_BANK)
                     nc.gpsimd.tensor_add(out=y[:, cols], in0=y[:, cols], in1=beta_all[:, cols])
                 nc.sync.dma_start(out=out_tiles[:, i, cols], in_=y[:, cols])
 
@@ -470,10 +486,12 @@ def tile_positionencoder_kernel(tc, state, W_words, W_scales, b, gamma, beta, ou
                     neg_mean = minus_mean_of_y(total_of(ahead[1]))
                 if step == 1:
                     minus_mean(total_of(FLIPPED_TILES[0]), neg_p_mean[:], 0.0)
-                if step == 2:
                     flipped_mean(0)
+                if step == 2:
+                    all_columns()
                     flipped_sums(0)
                     flipped_std(0)
+                    all_columns()
                 if step >= 3:
                     finish_blocks(2)
-                finish(i, current, current_rstd, not ahead)
+                finish(i, current, current_rstd, step == 0, not ahead)

@@ -381,7 +381,7 @@ def tile_positionencoder_kernel(tc, state, W_words, W_scales, b, gamma, beta, ou
                 stored = slice((blk - 1) * BANK, (blk + 1) * BANK)
                 nc.sync.dma_start(out=out_tiles[:, FLIPPED_TILES[q], stored], in_=result[:, stored])
 
-        def inverse_std(y, half, earlier):
+        def square(y, half):
             half_cols = N_OUT // 2
             squares = scratch.tile([P, half_cols], BF16, name="squares")
             sum_sq = stats.tile([P, 1], F32, name="sum_sq%d" % half)
@@ -389,13 +389,19 @@ def tile_positionencoder_kernel(tc, state, W_words, W_scales, b, gamma, beta, ou
                 out=squares[:], in_=y[:, half * half_cols : (half + 1) * half_cols],
                 func=ACT.Square, accum_out=sum_sq[:],
             )
-            answer = stats.tile([P, 1], F32, name="answer%d" % half)
+            return sum_sq
+
+        def inverse_std(sums):
+            part = stats.tile([P, 1], F32, name="part")
             nc.scalar.activation(
-                out=answer[:], in_=sum_sq[:], scale=1.0 / N_OUT,
-                func=ACT.Abs_reciprocal_sqrt if half else ACT.Identity,
-                bias=earlier[:, 0:1],
+                out=part[:], in_=sums[0][:], func=ACT.Identity, scale=1.0 / N_OUT, bias=eps[:, 0:1]
             )
-            return answer
+            rstd = stats.tile([P, 1], F32, name="rstd")
+            nc.scalar.activation(
+                out=rstd[:], in_=sums[1][:], func=ACT.Abs_reciprocal_sqrt, scale=1.0 / N_OUT,
+                bias=part[:, 0:1],
+            )
+            return rstd
 
         def centred(i, y, neg_mean, banks):
             for blk in banks:
@@ -459,7 +465,7 @@ def tile_positionencoder_kernel(tc, state, W_words, W_scales, b, gamma, beta, ou
             take_units(2)
             neg_mean = minus_mean_of_y(total)
             gamma_banks = spread_gamma()
-            rstd = inverse_std(y, 1, inverse_std(y, 0, eps))
+            rstd = inverse_std([square(y, half) for half in range(2)])
             blocks = list(range(BANKS))
 
             def finish_blocks(count):
@@ -471,19 +477,24 @@ def tile_positionencoder_kernel(tc, state, W_words, W_scales, b, gamma, beta, ou
             for step, i in enumerate(straight):
                 current, current_rstd = y, rstd
                 ahead = straight[step + 1 :]
-                take_units(1)
+                side_work = take_units if step < 3 else finish_blocks
+                if step != 3:
+                    side_work(1)
                 if ahead:
                     y = new_row_tile()
                     centred(ahead[0], y, neg_mean, range(BANKS // 2))
-                    half = inverse_std(y, 0, eps)
-                take_units(1)
+                    first_sum = square(y, 0)
+                if step != 3:
+                    side_work(1)
                 if ahead:
                     centred(ahead[0], y, neg_mean, range(BANKS // 2, BANKS))
-                    rstd = inverse_std(y, 1, half)
+                    second_sum = square(y, 1)
                 if step == 3:
                     flipped_turn()
                 if len(ahead) > 1:
                     neg_mean = minus_mean_of_y(total_of(ahead[1]))
+                if ahead:
+                    rstd = inverse_std([first_sum, second_sum])
                 if step == 1:
                     minus_mean(total_of(FLIPPED_TILES[0]), neg_p_mean[:], 0.0)
                     flipped_mean(0)
@@ -493,5 +504,5 @@ def tile_positionencoder_kernel(tc, state, W_words, W_scales, b, gamma, beta, ou
                     flipped_std(0)
                     all_columns()
                 if step >= 3:
-                    finish_blocks(2)
+                    side_work(1)
                 finish(i, current, current_rstd, step == 0, not ahead)

import math

import concourse.mybir as mybir
from concourse.masks import make_identity

F32 = mybir.dt.float32
BF16 = mybir.dt.bfloat16
I32 = mybir.dt.int32
U32 = mybir.dt.uint32
U8 = mybir.dt.uint8
FP8X4 = mybir.dt.float8_e4m3fn_x4
ALU = mybir.AluOpType
ACT = mybir.ActivationFunctionType
ACTIVATION = mybir.EngineType.Activation
DVE = mybir.EngineType.DVE
POOL = mybir.EngineType.Pool

P = 128
PACK = 4
ROWS = 1024
COORDS = 4
PER_COORD = 128
N_OUT = 4096
BANK = 512
ROW_TILES = ROWS // P
BANKS = N_OUT // BANK
GAIN_BANK = 1024
GROUPS = N_OUT // GAIN_BANK
PIECES = (slice(0, 128), slice(128, 256), slice(256, 512), slice(512, 768), slice(768, 1024))
FLIPPED_ROWS = PIECES[1]
FLIPPED_TILES = (1,)
FLIPPED_WIDTH = len(FLIPPED_TILES) * P
OUT_BLOCKS = N_OUT // P
UNIT = BANK // FLIPPED_WIDTH
PARTS = 3
MAX_COORD = 10.0
LN_EPS = 1e-5

FLOPS = 2 * ROWS * COORDS * PER_COORD * N_OUT


def tile_positionencoder_kernel(tc, state, W_words, W_scales, b, gamma, beta, out):
    nc = tc.nc
    with (
        tc.tile_pool(name="const", bufs=1) as const,
        tc.tile_pool(name="rows", bufs=5) as rows,
        tc.tile_pool(name="scratch", bufs=2) as scratch,
        tc.tile_pool(name="stats", bufs=4) as stats,
        tc.psum_pool(name="gain", bufs=1) as gain,
        tc.psum_pool(name="psum", bufs=3) as psum,
        tc.psum_pool(name="side", bufs=1) as side,
    ):
        state_sb = const.tile([P, ROW_TILES * COORDS], BF16)
        nc.sync.dma_start(out=state_sb[:], in_=state.rearrange("(m i) c -> m (i c)", i=ROW_TILES))

        by_block = const.tile([P, P], BF16)
        nc.vector.memset(by_block[:].bitcast(I32), 0)
        for slot, vector in enumerate((b, gamma, beta)):
            nc.sync.dma_start(
                out=by_block[slot * OUT_BLOCKS : (slot + 1) * OUT_BLOCKS, :],
                in_=vector.rearrange("(j p) -> j p", p=P),
            )

        w_scales = const.tile([P, N_OUT], U8, align_bytes=64)
        nc.vector.memset(w_scales[:].bitcast(I32), 0)
        for r in range(4):
            nc.sync.dma_start(
                out=w_scales[r:P:32, :].bitcast(I32), in_=W_scales[0, r:16:4, :].bitcast(I32)
            )

        w_codes = const.tile([P, N_OUT], U32, align_bytes=64)
        w_words = W_words[0].rearrange("p n t -> p (n t)").bitcast(I32)
        for piece in range(4):
            cols = slice(piece * 1024, (piece + 1) * 1024)
            nc.sync.dma_start(out=w_codes[:, cols].bitcast(I32), in_=w_words[:, cols])

        b_all = const.tile([P, N_OUT], BF16)
        nc.sync.dma_start(out=b_all[:], in_=b.partition_broadcast(P))
        beta_all = const.tile([P, N_OUT], BF16)
        nc.sync.dma_start(out=beta_all[:], in_=beta.partition_broadcast(P))

        k_index = const.tile([P, PACK], I32)
        nc.gpsimd.iota(k_index[:], pattern=[[1, PACK]], base=0, channel_multiplier=PACK)
        identity = const.tile([P, P], F32)
        make_identity(nc, identity[:])
        j_index = const.tile([P, PACK], I32)
        nc.vector.tensor_single_scalar(
            out=j_index[:], in_=k_index[:], scalar=PER_COORD - 1, op=ALU.bitwise_and
        )
        exponent = const.tile([P, PACK], F32)
        nc.vector.tensor_scalar_mul(out=exponent[:], in0=j_index[:], scalar1=-2.0 / PER_COORD)
        base = const.tile([P, PACK], F32)
        nc.gpsimd.memset(base[:], 10000.0)
        freq = const.tile([P, PACK], F32)
        nc.gpsimd.tensor_tensor(out=freq[:], in0=base[:], in1=exponent[:], op=ALU.pow)
        half_pi = const.tile([P, 1], F32)
        nc.vector.tensor_scalar(
            out=half_pi[:], in0=base[:, 0:1], scalar1=0.0, scalar2=math.pi / 2.0,
            op0=ALU.mult, op1=ALU.add,
        )
        eps = const.tile([P, 1], F32)
        nc.vector.tensor_scalar(
            out=eps[:], in0=base[:, 0:1], scalar1=0.0, scalar2=LN_EPS, op0=ALU.mult, op1=ALU.add
        )
        warm = const.tile([P, 1], F32)
        nc.scalar.activation(out=warm[:], in_=half_pi[:], func=ACT.Sin)

        s_low = const.tile([P, ROW_TILES * COORDS], F32)
        nc.vector.tensor_scalar(
            out=s_low[:], in0=state_sb[:], scalar1=1.0 / MAX_COORD, scalar2=0.0,
            op0=ALU.mult, op1=ALU.max,
        )
        s_wide = const.tile([P, ROW_TILES * COORDS, P // COORDS], F32)
        nc.vector.tensor_scalar_min(
            out=s_wide[:],
            in0=s_low[:].unsqueeze(2).to_broadcast([P, ROW_TILES * COORDS, P // COORDS]),
            scalar1=1.0,
        )

        identity_bf16 = const.tile([P, P], BF16)
        nc.vector.tensor_copy(out=identity_bf16[:], in_=identity[:])
        ones = const.tile([P, P], BF16)
        nc.vector.memset(ones[:], 1.0)
        vectors = const.tile([P, N_OUT], BF16)
        nc.gpsimd.memset(vectors[:].bitcast(I32), 0)
        nc.sync.dma_start(out=vectors[0:PARTS, :], in_=gamma.partition_broadcast(PARTS))
        nc.sync.dma_start(out=vectors[PARTS : 2 * PARTS, :], in_=beta.partition_broadcast(PARTS))
        split = const.tile([P, len(FLIPPED_TILES), P], BF16)
        nc.gpsimd.memset(split[:].bitcast(I32), 0)

        pe_planes = const.tile([P, PACK, ROWS], BF16)
        pe_grouped = const.tile([P, ROWS, PACK], BF16, align_bytes=64)
        pe_codes = const.tile([P, ROWS], U32, align_bytes=64)
        pe_scales = const.tile([P, ROWS], U8, align_bytes=64)

        def turn_state(cols, pool, tag):
            count = cols.stop - cols.start
            s_t = pool.tile([P, count], F32, tag=tag, name="s_t")
            for q in range(count // P):
                i = cols.start // P + q
                nc.tensor.transpose(
                    s_t[:, q * P : (q + 1) * P],
                    s_wide[:, i * COORDS : (i + 1) * COORDS, :].rearrange("m c e -> m (c e)"),
                    identity[:],
                )
            return s_t

        def encode(cols, s_t):
            for t in range(PACK):
                nc.scalar.activation(
                    out=pe_planes[:, t, cols], in_=s_t[:], func=ACT.Sin,
                    scale=freq[:, t : t + 1], bias=half_pi[:, 0:1] if t % 2 else 0.0,
                )

        def quantise(cols):
            nc.vector.tensor_copy(
                out=pe_grouped[:, cols, :], in_=pe_planes[:, :, cols].rearrange("p t r -> p r t")
            )
            nc.vector.quantize_mx(
                out=pe_codes[:, cols].bitcast(FP8X4),
                scales=pe_scales[:, cols],
                in_=pe_grouped[:, cols, :].rearrange("p r t -> p (r t)"),
            )

        vectors_bf16 = const.tile([P, 3, OUT_BLOCKS], BF16)
        b_cols = const.tile([P, OUT_BLOCKS], F32)
        gamma_cols = const.tile([P, OUT_BLOCKS], F32)
        b_gamma_cols = const.tile([P, OUT_BLOCKS], F32)
        b_centred_cols = const.tile([P, OUT_BLOCKS], F32)
        neg_b_share = const.tile([P, 1], F32)
        neg_b_mean = const.tile([P, 1], F32)

        def turn_vectors():
            cols_t = side.tile([P, P], BF16, tag="side", name="cols_t")
            nc.tensor.transpose(cols_t[:], by_block[:], identity_bf16[:])
            nc.vector.tensor_copy(
                out=vectors_bf16[:].rearrange("p v j -> p (v j)"), in_=cols_t[:, : 3 * OUT_BLOCKS]
            )
            nc.vector.tensor_copy(out=b_cols[:], in_=cols_t[:, :OUT_BLOCKS])
            nc.vector.tensor_copy(out=gamma_cols[:], in_=cols_t[:, OUT_BLOCKS : 2 * OUT_BLOCKS])

        def mean_of_b():
            b_sums = side.tile([P, OUT_BLOCKS], F32, tag="side", name="b_sums")
            nc.tensor.matmul(out=b_sums[:], lhsT=ones[:], rhs=vectors_bf16[:, 0, :], start=True, stop=True)
            b_ignored = const.tile([P, OUT_BLOCKS], F32)
            nc.scalar.activation(
                out=b_ignored[:], in_=b_sums[:], func=ACT.Copy, scale=-1.0 / (N_OUT * BANK),
                accum_out=neg_b_share[:],
            )

        def flipped_constants():
            nc.vector.tensor_mul(out=b_gamma_cols[:], in0=b_cols[:], in1=gamma_cols[:])
            nc.vector.tensor_scalar_mul(
                out=neg_b_mean[:], in0=neg_b_share[:], scalar1=float(BANK)
            )
            nc.vector.tensor_scalar_add(
                out=b_centred_cols[:], in0=b_cols[:], scalar1=neg_b_mean[:, 0:1]
            )

        gamma_tags = ["gamma_bank%d" % g for g in range(GROUPS)]

        def spread_gamma():
            banks = []
            for g in range(GROUPS):
                gamma_bank = gain.tile([P, GAIN_BANK], BF16, tag=gamma_tags[g], name="gamma_bank")
                spread(gamma_bank, 1, g)
                banks.append(gamma_bank)
            return banks

        def spread(bank, vector, g):
            for h in range(GAIN_BANK // P):
                j = g * (GAIN_BANK // P) + h
                nc.tensor.transpose(
                    bank[:, h * P : (h + 1) * P],
                    vectors_bf16[:, vector, j : j + 1].to_broadcast([P, P]),
                    identity_bf16[:],
                )

        out_tiles = out.rearrange("(m i) n -> m i n", i=ROW_TILES)
        groups = [slice(g * GAIN_BANK, (g + 1) * GAIN_BANK) for g in range(GROUPS)]

        def multiply(acc, i, blk, start, stop):
            tile_rows = slice(i * P, (i + 1) * P)
            cols = slice(blk * BANK, (blk + 1) * BANK)
            nc.tensor.matmul_mx(
                out=acc[:],
                lhsT=pe_codes[:, tile_rows].bitcast(FP8X4),
                lhsT_scale=pe_scales[:, tile_rows],
                rhs=w_codes[:, cols].bitcast(FP8X4),
                rhs_scale=w_scales[:, cols],
                start=start,
                stop=stop,
            )

        def total_of(i, early_bank=None):
            if early_bank is None:
                total = psum.tile([P, BANK], F32, tag="bank", name="total")
            else:
                total = gain.tile([P, BANK], F32, tag=early_bank, name="early_total")
            for blk in range(BANKS):
                multiply(total, i, blk, blk == 0, blk == BANKS - 1)
            return total

        def minus_mean(total, neg_mean, share):
            ignored = scratch.tile([P, BANK], BF16, name="ignored")
            nc.scalar.activation(
                out=ignored[:], in_=total[:], func=ACT.Identity, scale=-1.0 / N_OUT,
                bias=share, accum_out=neg_mean,
            )

        def minus_mean_of_y(total):
            neg_mean = stats.tile([P, 1], F32, name="neg_mean")
            minus_mean(total, neg_mean[:], neg_b_share[:, 0:1])
            return neg_mean

        scaled = const.tile([P, OUT_BLOCKS, FLIPPED_WIDTH], F32)
        squared = const.tile([P, OUT_BLOCKS, FLIPPED_WIDTH], F32)

        def flipped_products(unit):
            pool, tag = (gain, gamma_tags[0]) if unit == 1 else (side, "side")
            acc = pool.tile([P, UNIT, FLIPPED_WIDTH], F32, tag=tag, name="flipped_acc")
            for h in range(UNIT):
                j = UNIT * unit + h
                cols = slice(j * P, (j + 1) * P)
                nc.tensor.matmul_mx(
                    out=acc[:, h, :],
                    lhsT=w_codes[:, cols].bitcast(FP8X4),
                    lhsT_scale=w_scales[:, cols],
                    rhs=pe_codes[:, FLIPPED_ROWS].bitcast(FP8X4),
                    rhs_scale=pe_scales[:, FLIPPED_ROWS],
                    start=True,
                    stop=True,
                )
            for h in range(UNIT):
                j = UNIT * unit + h
                nc.scalar.activation(
                    out=squared[:, j, :], in_=acc[:, h, :], func=ACT.Square,
                    bias=b_centred_cols[:, j : j + 1],
                )
                next_column()
                nc.scalar.activation(
                    out=scaled[:, j, :], in_=acc[:, h, :], func=ACT.Identity,
                    scale=gamma_cols[:, j : j + 1], bias=b_gamma_cols[:, j : j + 1],
                )
                next_column()

        neg_p_mean = const.tile([P, len(FLIPPED_TILES)], F32)
        flipped_rstd = const.tile([P, len(FLIPPED_TILES)], F32)

        mean_sq = const.tile([P, len(FLIPPED_TILES)], F32)
        rest = const.tile([P, PARTS + 3, 2], F32)
        split_t = const.tile([P, len(FLIPPED_TILES), P], BF16)

        def flipped_sums(q):
            sums = side.tile([P, P], F32, tag="side", name="sums")
            for j in range(OUT_BLOCKS):
                nc.tensor.matmul(
                    out=sums[:], lhsT=squared[:, j, q * P : (q + 1) * P], rhs=identity[:],
                    is_transpose=True, start=(j == 0), stop=(j == OUT_BLOCKS - 1),
                )
            ignored = scratch.tile([P, BANK], BF16, name="ignored")
            nc.scalar.activation(
                out=ignored[:, :P], in_=sums[:], func=ACT.Copy, scale=1.0 / N_OUT,
                accum_out=mean_sq[:, q : q + 1],
            )

        waiting = []

        def next_column():
            for call in waiting[:1]:
                call()
            for call in waiting[:1]:
                waiting.remove(call)

        def all_columns():
            for call in waiting:
                call()
            waiting.clear()

        def put(out_col, in_col, func=ACT.Identity, scale=1.0, bias=0.0):
            waiting.append(
                lambda: nc.scalar.activation(
                    out=out_col, in_=in_col, func=func, scale=scale, bias=bias
                )
            )

        def split_value(q, v):
            for s in range(PARTS):
                part = split[:, q, v * PARTS + s : v * PARTS + s + 1]
                left = rest[:, s, v : v + 1]
                put(part, left, func=ACT.Copy)
                if s + 1 < PARTS:
                    put(rest[:, s + 1, v : v + 1], part, scale=-1.0, bias=left)

        def flipped_mean(q):
            mean = neg_p_mean[:, q : q + 1]
            p_mean = rest[:, PARTS, 0:1]
            put(rest[:, 0, 0:1], mean, bias=neg_b_mean[:, 0:1])
            put(p_mean, mean, func=ACT.Copy, scale=-1.0)
            split_value(q, 0)
            put(rest[:, PARTS + 1, 0:1], mean, scale=p_mean, bias=eps[:, 0:1])

        def flipped_std(q):
            eps_less = rest[:, PARTS + 1, 0:1]
            rstd = flipped_rstd[:, q : q + 1]
            mean_square = mean_sq[:, q : q + 1]
            put(rstd, mean_square, func=ACT.Abs_reciprocal_sqrt, bias=eps_less)
            put(rest[:, PARTS + 2, 0:1], mean_square, bias=eps_less)
            put(rest[:, 0, 1:2], rest[:, PARTS + 2, 0:1], scale=rstd)
            split_value(q, 1)

        def flipped_turn():
            for q in range(len(FLIPPED_TILES)):
                turned = side.tile([P, P], BF16, tag="side", name="turned")
                nc.tensor.transpose(turned[:], split[:, q, :], identity_bf16[:])
                nc.scalar.copy(out=split_t[:, q, :], in_=turned[:])

        results = {}

        def flipped_finish(q, blk, on_vector):
            if blk == 0:
                results[q] = rows.tile([P, N_OUT], F32, tag="y", name="result")
            result = results[q]
            cols = slice(blk * BANK, (blk + 1) * BANK)
            acc = side.tile([P, BANK], F32, tag="side", name="turned_acc")
            nc.tensor.matmul(
                out=acc[:], lhsT=split_t[:, q, :], rhs=vectors[:, cols], start=True, stop=False
            )
            for h in range(BANK // P):
                nc.tensor.matmul(
                    out=acc[:, h * P : (h + 1) * P],
                    lhsT=scaled[:, blk * (BANK // P) + h, q * P : (q + 1) * P],
                    rhs=identity[:], is_transpose=True, start=False, stop=(h == BANK // P - 1),
                )
            rstd = flipped_rstd[:, q : q + 1]
            if on_vector:
                nc.vector.tensor_scalar_mul(out=result[:, cols], in0=acc[:], scalar1=rstd)
            else:
                nc.scalar.mul(out=result[:, cols], in_=acc[:], mul=rstd)
            if blk % 2 == 1:
                stored = slice((blk - 1) * BANK, (blk + 1) * BANK)
                nc.sync.dma_start(out=out_tiles[:, FLIPPED_TILES[q], stored], in_=result[:, stored])

        def square(y, half):
            half_cols = N_OUT // 2
            squares = scratch.tile([P, half_cols], BF16, name="squares")
            sum_sq = stats.tile([P, 1], F32, name="sum_sq%d" % half)
            nc.scalar.activation(
                out=squares[:], in_=y[:, half * half_cols : (half + 1) * half_cols],
                func=ACT.Square, accum_out=sum_sq[:],
            )
            return sum_sq

        def inverse_std(sums):
            part = stats.tile([P, 1], F32, name="part")
            nc.scalar.activation(
                out=part[:], in_=sums[0][:], func=ACT.Identity, scale=1.0 / N_OUT, bias=eps[:, 0:1]
            )
            rstd = stats.tile([P, 1], F32, name="rstd")
            nc.scalar.activation(
                out=rstd[:], in_=sums[1][:], func=ACT.Abs_reciprocal_sqrt, scale=1.0 / N_OUT,
                bias=part[:, 0:1],
            )
            return rstd

        def centred(i, y, neg_mean, banks):
            for blk in banks:
                cols = slice(blk * BANK, (blk + 1) * BANK)
                acc = psum.tile([P, BANK], F32, tag="bank", name="acc")
                multiply(acc, i, blk, True, True)
                nc.vector.scalar_tensor_tensor(
                    out=y[:, cols], in0=acc[:], scalar=neg_mean[:, 0:1], in1=b_all[:, cols],
                    op0=ALU.add, op1=ALU.add,
                )

        def new_row_tile():
            y = rows.tile([P, N_OUT], F32, tag="y", name="y")
            return y

        def finish(i, y, rstd, first, last):
            for g, cols in enumerate(groups):
                nc.vector.scalar_tensor_tensor(
                    out=y[:, cols], in0=y[:, cols], scalar=rstd[:, 0:1],
                    in1=gamma_banks[g][:], op0=ALU.mult, op1=ALU.mult,
                )
                if last and g > 0:
                    beta_bank = psum.tile([P, GAIN_BANK], BF16, tag="bank", name="beta_bank")
                    spread(beta_bank, 2, g)
                    nc.vector.tensor_add(out=y[:, cols], in0=y[:, cols], in1=beta_bank[:])
                elif first or last:
                    nc.gpsimd.tensor_add(out=y[:, cols], in0=y[:, cols], in1=beta_all[:, cols])
                else:
                    if g % 2 == 0:
                        continue
                    cols = slice((g - 1) * GAIN_BANK, (g + 1) * GAIN_BANK)
                    nc.gpsimd.tensor_add(out=y[:, cols], in0=y[:, cols], in1=beta_all[:, cols])
                nc.sync.dma_start(out=out_tiles[:, i, cols], in_=y[:, cols])

        straight = [i for i in range(ROW_TILES) if i not in FLIPPED_TILES]
        units = list(range(OUT_BLOCKS // UNIT))

        def take_units(count):
            for unit in units[:count]:
                flipped_products(unit)
            for unit in units[:count]:
                units.remove(unit)

        with tc.manual_schedule(engines={ACTIVATION, DVE, POOL}):
            banks = [(psum, "bank")] * 3 + [(gain, gamma_tags[0]), (gain, gamma_tags[1])]
            turned = [turn_state(cols, *bank) for cols, bank in zip(PIECES, banks)]
            encode(PIECES[0], turned[0])
            turn_vectors()
            quantise(PIECES[0])
            total = total_of(straight[0], gamma_tags[2])
            mean_of_b()
            for cols, s_t in zip(PIECES[1:], turned[1:]):
                encode(cols, s_t)
                quantise(cols)
            flipped_constants()
            nc.scalar.activation(out=warm[:], in_=half_pi[:], func=ACT.Abs_reciprocal_sqrt)
            neg_mean = minus_mean_of_y(total)
            y = new_row_tile()
            centred(straight[0], y, neg_mean, range(BANKS))
            total = total_of(straight[1], gamma_tags[3])
            take_units(2)
            neg_mean = minus_mean_of_y(total)
            gamma_banks = spread_gamma()
            rstd = inverse_std([square(y, half) for half in range(2)])
            blocks = list(range(BANKS))

            def finish_blocks(count):
                for blk in blocks[:count]:
                    flipped_finish(0, blk, False)
                for blk in blocks[:count]:
                    blocks.remove(blk)

            for step, i in enumerate(straight):
                current, current_rstd = y, rstd
                ahead = straight[step + 1 :]
                side_work = take_units if step < 3 else finish_blocks
                if step != 3:
                    side_work(1)
                if ahead:
                    y = new_row_tile()
                    centred(ahead[0], y, neg_mean, range(BANKS // 2))
                    first_sum = square(y, 0)
                if step != 3:
                    side_work(1)
                if ahead:
                    centred(ahead[0], y, neg_mean, range(BANKS // 2, BANKS))
                    second_sum = square(y, 1)
                if step == 3:
                    flipped_turn()
                if len(ahead) > 1:
                    neg_mean = minus_mean_of_y(total_of(ahead[1]))
                if ahead:
                    rstd = inverse_std([first_sum, second_sum])
                if step == 1:
                    minus_mean(total_of(FLIPPED_TILES[0]), neg_p_mean[:], 0.0)
                    flipped_mean(0)
                if step == 2:
                    all_columns()
                    flipped_sums(0)
                    flipped_std(0)
                    all_columns()
                if step >= 3:
                    side_work(1)
                finish(i, current, current_rstd, step == 0, not ahead)
